import numpy as np
import ml_dtypes


def mxq(x, axis, fmt="e4m3"):
    dtype, down = {"e4m3": (ml_dtypes.float8_e4m3fn, 7), "e5m2": (ml_dtypes.float8_e5m2, 14)}[fmt]
    v = np.moveaxis(np.asarray(x, np.float32).astype(ml_dtypes.bfloat16).astype(np.float64), axis, -1)
    blocks = v.reshape(v.shape[:-1] + (-1, 32))
    amax = np.abs(blocks).max(-1, keepdims=True)
    byte = np.maximum(np.where(amax > 0, np.frexp(amax)[1] - 1 + 127, 0) - down, 1)
    scale = np.exp2(byte - 127.0)
    codes = (blocks / scale).astype(np.float32).astype(dtype).astype(np.float64)
    return np.moveaxis((codes * scale).reshape(v.shape), -1, axis)


WIDE = False


def mx_kscale(k):
    if not WIDE:
        return np.ones(k)
    levels = np.array([10, -10, 5, -5, 0])
    if k % 512:
        return np.exp2(np.random.permutation(np.resize(levels, k // 32))).repeat(32)
    a = np.empty((k // 512, 16))
    for p in range(k // 512):
        a[p, :8] = np.random.permutation(np.resize(levels, 8))
        for g in range(8):
            far = levels[np.abs(levels - a[p, g]) >= 10]
            a[p, g + 8] = far[np.random.randint(len(far))]
    return np.exp2(a.ravel()).repeat(32)


BF16 = ml_dtypes.bfloat16


def bf(x):
    return np.asarray(x, np.float32).astype(BF16)


def f64(x):
    return np.asarray(x).astype(np.float64)


B, IN, H = 2048, 512, 512
G = 4 * H
EPS = 1e-5


def _layernorm(v, gamma, beta):
    mean = np.mean(v, axis=-1, keepdims=True)
    var = np.mean(np.square(v - mean), axis=-1, keepdims=True)
    return (v - mean) / np.sqrt(var + EPS) * gamma + beta


def sigmoid(v):
    return 1.0 / (1.0 + np.exp(-v))


def setup_inputs():
    s, t = mx_kscale(IN), mx_kscale(H)
    return {
        "x": bf(np.random.standard_normal((B, IN)) * s),
        "h_prev": bf(np.random.standard_normal((B, H)) * t),
        "c_prev": bf(np.random.standard_normal((B, H))),
        "W_ih": bf(np.random.standard_normal((IN, G)) / np.sqrt(IN) / s[:, None]),
        "W_hh": bf(np.random.standard_normal((H, G)) / np.sqrt(H) / t[:, None]),
        "gamma_ih": bf(1.0 + 0.2 * np.random.standard_normal(G)),
        "beta_ih": bf(0.3 * np.random.standard_normal(G)),
        "gamma_hh": bf(1.0 + 0.2 * np.random.standard_normal(G)),
        "beta_hh": bf(0.3 * np.random.standard_normal(G)),
        "gamma_c": bf(1.0 + 0.2 * np.random.standard_normal(H)),
        "beta_c": bf(0.3 * np.random.standard_normal(H)),
    }


def reference(x, h_prev, c_prev, W_ih, W_hh, gamma_ih, beta_ih, gamma_hh, beta_hh, gamma_c, beta_c):
    a_ih = mxq(f64(x), 1, "e4m3") @ mxq(f64(W_ih), 0, "e4m3")
    a_hh = mxq(f64(h_prev), 1, "e4m3") @ mxq(f64(W_hh), 0, "e4m3")
    gates_ih = _layernorm(a_ih, f64(gamma_ih), f64(beta_ih))
    gates_hh = _layernorm(a_hh, f64(gamma_hh), f64(beta_hh))
    gates = gates_ih + gates_hh
    i_g, f_g, g_g, o_g = np.split(gates, 4, axis=1)
    i_t = sigmoid(i_g)
    f_t = sigmoid(f_g)
    g_t = np.tanh(g_g)
    o_t = sigmoid(o_g)
    c_t = f_t * f64(c_prev) + i_t * g_t
    h_t = o_t * np.tanh(_layernorm(c_t, f64(gamma_c), f64(beta_c)))
    return (h_t, c_t)

@@ -1,0 +1,511 @@
+from contextlib import ExitStack
+
+import concourse.mybir as mybir
+from concourse.masks import make_identity
+
+F32 = mybir.dt.float32
+BF16 = mybir.dt.bfloat16
+U32 = mybir.dt.uint32
+U8 = mybir.dt.uint8
+FP8X4 = mybir.dt.float8_e4m3fn_x4
+ALU = mybir.AluOpType
+ACT = mybir.ActivationFunctionType
+AX = mybir.AxisListType
+
+P = 128
+B = 2048
+K = 512
+H = 512
+G = 2048
+NT = B // P
+GRP = 4
+EPS = 1e-5
+FLOPS = 2 * 2 * B * K * G
+GATE = {"i": 0, "f": 1, "g": 2}
+TCOLS = 3 * H
+ENGINES = ("PE", "S", "V", "G", "SP")
+ACC_BUFS = 4
+TP_BUFS = 3
+S_BUFS = 3
+
+ORDER = {
+    "PE": (
+        ("fwd", -2, "g"), ("main", 0, 6), ("main", 0, 7), ("mean", 1, 0),
+        ("fwd", -2, "f"), ("fwd", -2, "i"), ("main", 1, 0), ("main", 1, 1),
+        ("main", 1, 2), ("xt", 2, None), ("main", 1, 3), ("mean", 1, 1),
+        ("main", 1, 4), ("cb", -3, None), ("cpt", -2, None), ("main", 1, 5),
+    ),
+    "S": (
+        ("nm", 1, 0), ("sq", 1, 0), ("sq", 1, 1), ("act", -2, "i"),
+        ("sq", 1, 2), ("sq", 1, 3), ("xcopy", 2, None), ("nm", 1, 1),
+        ("tanh", -6, None), ("nmc", -4, None), ("red", 0, 0), ("sq", 1, 4),
+        ("sq", 1, 5), ("cstat", -4, None), ("ccopy", -3, None), ("acto", -3, None),
+        ("sq", 1, 6), ("sq", 1, 7), ("act", -1, "g"), ("red", 0, 1),
+        ("act", -1, "f"),
+    ),
+    "V": (
+        ("apply", 1, 0), ("apply", 1, 1), ("rs", -1, 1), ("apply", 1, 2),
+        ("apply", 1, 3), ("LN", -5, None), ("xq", 2, None), ("h", -6, None),
+        ("p", -2, None), ("q", -2, None), ("apply", 1, 4), ("apply", 1, 5),
+        ("uo", -1, None), ("apply", 1, 6), ("apply", 1, 7), ("rs", 0, 0),
+    ),
+    "G": (
+        ("rc", -4, None), ("r", 0, 1), ("r", 1, 0),
+    ),
+    "SP": (
+        ("ld", 6, None), ("stc", -3, None), ("sth", -6, None),
+    ),
+}
+
+
+def tile_layernormlstmcell_kernel(
+    tc, x, h_prev, c_prev, W_ih, W_hh, gamma_ih, beta_ih, gamma_hh, beta_hh, gamma_c, beta_c, out_0, out_1
+):
+    nc = tc.nc
+    x_v = x.rearrange("(p t) k -> p t k", t=NT)
+    h_v = h_prev.rearrange("(p t) k -> p t k", t=NT)
+    c_v = c_prev.rearrange("(p t) k -> p t k", t=NT)
+    ho_v = out_0.rearrange("(p t) k -> p t k", t=NT)
+    co_v = out_1.rearrange("(p t) k -> p t k", t=NT)
+
+    with ExitStack() as ctx:
+        const = ctx.enter_context(tc.tile_pool(name="const", bufs=1))
+        io = ctx.enter_context(tc.tile_pool(name="io", bufs=2))
+        xp = ctx.enter_context(tc.tile_pool(name="xp", bufs=4))
+        prep = ctx.enter_context(tc.tile_pool(name="prep", bufs=4))
+        work = ctx.enter_context(tc.tile_pool(name="work", bufs=2))
+        small = ctx.enter_context(tc.tile_pool(name="small", bufs=4))
+        ps_acc = ctx.enter_context(tc.psum_pool(name="ps_acc", bufs=ACC_BUFS))
+        ps_tp = ctx.enter_context(tc.psum_pool(name="ps_tp", bufs=TP_BUFS))
+        ps_mean = ctx.enter_context(tc.psum_pool(name="ps_mean", bufs=1))
+        ctx.enter_context(tc.manual_schedule())
+
+        ident = const.tile([P, P], F32, name="ident")
+        make_identity(nc, ident[:])
+        neghalf = const.tile([P, 1], F32, name="neghalf")
+        nc.gpsimd.memset(neghalf[:], -0.5)
+        identb = const.tile([P, P], BF16, name="identb")
+        nc.vector.tensor_copy(out=identb[:], in_=ident[:])
+        junkm = const.tile([P, P], F32, name="junkm")
+        junkv = const.tile([P, P], F32, name="junkv")
+        junkc = const.tile([P, H], F32, name="junkc")
+        wc = [const.tile([P, G], U32, name="wc%d" % m, align_bytes=64) for m in range(2)]
+        ws = [const.tile([P, G], U8, name="ws%d" % m, align_bytes=64) for m in range(2)]
+        gam = [const.tile([P, G], BF16, name="gam%d" % m) for m in range(2)]
+        gamc = const.tile([P, H], BF16, name="gamc")
+        betc = const.tile([P, H], BF16, name="betc")
+        cin = const.tile([P, NT, H], BF16, name="cin")
+        bt32 = const.tile([P, P], F32, name="bt32")
+        betaT = const.tile([P, G // P], F32, name="betaT")
+        bso = const.tile([P, H], F32, name="bso")
+
+        T = {}
+
+        def load_group(g):
+            for nm_, view in (("xin", x_v), ("hin", h_v)):
+                til = io.tile([P, GRP, K], BF16, name=nm_)
+                nc.sync.dma_start(out=til[:], in_=view[:, g * GRP:(g + 1) * GRP, :])
+                T[(nm_, g)] = til
+
+        first = {}
+        for nm_, view in (("xin", x_v), ("hin", h_v)):
+            first[nm_] = io.tile([P, GRP, K], BF16, name=nm_)
+            nc.sync.dma_start(out=first[nm_][:, 0:2, :], in_=view[:, 0:2, :])
+            T[(nm_, 0)] = first[nm_]
+        ba = prep.tile([16, P], BF16, name="ba", bufs=1)
+        bb = prep.tile([16, P], BF16, name="bb", bufs=1)
+        nc.scalar.dma_start(out=ba[:], in_=beta_ih.rearrange("(r c) -> r c", c=P))
+        nc.scalar.dma_start(out=bb[:], in_=beta_hh.rearrange("(r c) -> r c", c=P))
+        raws = []
+        for m, W in enumerate((W_ih, W_hh)):
+            for hf in range(2):
+                raw = prep.tile([P, 4, 1024], BF16, name="raw")
+                nc.sync.dma_start(
+                    out=raw[:], in_=W[:, hf * 1024:(hf + 1) * 1024].rearrange("(p e) c -> p e c", e=4)
+                )
+                raws.append(raw)
+            nc.sync.dma_start(out=gam[m][:], in_=(gamma_ih, gamma_hh)[m].partition_broadcast(P))
+        for nm_, view in (("xin", x_v), ("hin", h_v)):
+            nc.sync.dma_start(out=first[nm_][:, 2:GRP, :], in_=view[:, 2:GRP, :])
+        nc.sync.dma_start(out=cin[:], in_=c_v)
+        load_group(1)
+        bo1 = prep.tile([P, H], BF16, name="bo1", bufs=1)
+        bo2 = prep.tile([P, H], BF16, name="bo2", bufs=1)
+        nc.sync.dma_start(out=bo1[:], in_=beta_ih[TCOLS:G].partition_broadcast(P))
+        nc.sync.dma_start(out=bo2[:], in_=beta_hh[TCOLS:G].partition_broadcast(P))
+        nc.sync.dma_start(out=gamc[:], in_=gamma_c.partition_broadcast(P))
+        nc.sync.dma_start(out=betc[:], in_=beta_c.partition_broadcast(P))
+
+        nc.vector.memset(bt32[:], 0.0)
+        nc.vector.tensor_tensor(out=bt32[0:16, :], in0=ba[:], in1=bb[:], op=ALU.add)
+        tpb = ps_tp.tile([P, 4, P], F32, name="tp")
+        nc.tensor.transpose(tpb[:, 0, :], bt32[:], ident[:])
+        nc.vector.tensor_copy(out=betaT[:], in_=tpb[:, 0, 0:G // P])
+
+        def e_wcopy(eng, u):
+            grp = prep.tile([P, 512, 4], BF16, name="grp", align_bytes=64)
+            dst = grp[:].rearrange("p (c i) t -> p c t i", i=4)
+            src = raws[u // 2][:, :, (u % 2) * 512:(u % 2 + 1) * 512].rearrange("p t (c i) -> p c t i", i=4)
+            if eng == "V":
+                nc.vector.tensor_copy(out=dst, in_=src)
+            else:
+                nc.scalar.copy(out=dst, in_=src)
+            T[("grp", u)] = grp
+
+        def e_wq(eng, u):
+            m = u // 4
+            c0 = (u % 4) * 512
+            nc.vector.quantize_mx(
+                out=wc[m][:, c0:c0 + 512].bitcast(FP8X4),
+                scales=ws[m][:, c0:c0 + 512],
+                in_=T[("grp", u)][:].rearrange("p c t -> p (c t)"),
+            )
+
+        def e_ld(eng, t):
+            load_group(t // GRP)
+
+        def e_xt(eng, t):
+            xt = ps_tp.tile([P, 4, P], F32, name="tp")
+            for o, nm_ in enumerate(("xin", "hin")):
+                src = T[(nm_, t // GRP)]
+                words = src[:, t % GRP, :].bitcast(F32)
+                for u in range(2):
+                    nc.tensor.transpose(xt[:, 2 * o + u, :], words[:, u:2 * P:2], ident[:])
+            T[("xt", t)] = xt
+
+        def e_xcopy(eng, t):
+            gx = xp.tile([P, 2, P, 2], F32, name="gx", bufs=2, align_bytes=64)
+            src = T[("xt", t)][:].rearrange("p (o u) r -> p o r u", u=2)
+            if eng == "V":
+                nc.vector.tensor_copy(out=gx[:], in_=src)
+            else:
+                nc.scalar.copy(out=gx[:], in_=src)
+            T[("gx", t)] = gx
+
+        def e_xq(eng, t):
+            xc = xp.tile([P, 2 * P], U32, name="xc", align_bytes=64)
+            xs = xp.tile([P, 2 * P], U8, name="xs", align_bytes=64)
+            nc.vector.quantize_mx(
+                out=xc[:].bitcast(FP8X4),
+                scales=xs[:],
+                in_=T[("gx", t)][:].rearrange("p o r u -> p (o r u)").bitcast(BF16),
+            )
+            T[("xc", t)] = xc
+            T[("xs", t)] = xs
+
+        def mx(out, t, m, cols, start, stop):
+            nc.tensor.matmul_mx(
+                out=out,
+                lhsT=T[("xc", t)][:, m * P:(m + 1) * P].bitcast(FP8X4),
+                lhsT_scale=T[("xs", t)][:, m * P:(m + 1) * P],
+                rhs=wc[m][:, cols].bitcast(FP8X4),
+                rhs_scale=ws[m][:, cols],
+                start=start,
+                stop=stop,
+            )
+
+        def e_mean(eng, t, m):
+            mp = ps_mean.tile([P, P], F32, name="mean_ps")
+            for j in range(G // P):
+                mx(mp[:], t, m, slice(j * P, (j + 1) * P), j == 0, j == G // P - 1)
+            T[("mean", t, m)] = mp
+
+        def e_nm(eng, t, m):
+            nm = small.tile([P, 1], F32, name="nm")
+            if eng == "V":
+                nc.vector.tensor_scalar(
+                    out=junkv[:], in0=T[("mean", t, m)][:], scalar1=-1.0 / G, scalar2=0.0, op0=ALU.mult, op1=ALU.add,
+                    accum_out=nm[:],
+                )
+            else:
+                nc.scalar.activation(
+                    out=junkm[:], in_=T[("mean", t, m)][:], func=ACT.Identity, scale=-1.0 / G, accum_out=nm[:]
+                )
+            T[("nm", t, m)] = nm
+
+        def e_main(eng, t, mk):
+            m, k = mk // 4, mk % 4
+            acc = ps_acc.tile([P, 512], F32, name="acc")
+            mx(acc[:], t, m, slice(k * 512, (k + 1) * 512), True, True)
+            T[("acc", t, mk)] = acc
+
+        def e_sq(eng, t, mk):
+            m, k = mk // 4, mk % 4
+            if k == 0:
+                T[("ssq", t, m)] = small.tile([P, 4], F32, name="ssq")
+                T[("s", t, m)] = work.tile([P, G], F32, name="s%d" % m, bufs=S_BUFS)
+            nc.scalar.activation(
+                out=T[("s", t, m)][:, k * 512:(k + 1) * 512], in_=T[("acc", t, mk)][:], func=ACT.Square,
+                bias=T[("nm", t, m)][:], scale=1.0, accum_out=T[("ssq", t, m)][:, k:k + 1],
+            )
+
+        def e_apply(eng, t, mk):
+            m, k = mk // 4, mk % 4
+            cols = slice(k * 512, (k + 1) * 512)
+            nc.vector.scalar_tensor_tensor(
+                out=T[("s", t, m)][:, cols], in0=T[("acc", t, mk)][:], scalar=T[("nm", t, m)][:],
+                in1=gam[m][:, cols], op0=ALU.add, op1=ALU.mult,
+            )
+
+        def e_red(eng, t, m):
+            ssum = small.tile([P, 1], F32, name="ssum")
+            if eng == "V":
+                nc.vector.tensor_reduce(out=ssum[:], in_=T[("ssq", t, m)][:], axis=AX.X, op=ALU.add)
+            else:
+                nc.scalar.activation(out=junkm[:, 0:4], in_=T[("ssq", t, m)][:], func=ACT.Identity, accum_out=ssum[:])
+            T[("ssum", t, m)] = ssum
+
+        def rstd(sumsq, count, nm_):
+            var = small.tile([P, 1], F32, name="var" + nm_)
+            nc.gpsimd.tensor_scalar(out=var[:], in0=sumsq[:], scalar1=1.0 / count, scalar2=EPS, op0=ALU.mult, op1=ALU.add)
+            r = small.tile([P, 1], F32, name="r" + nm_, bufs=6)
+            nc.gpsimd.tensor_tensor(out=r[:], in0=var[:], in1=neghalf[:], op=ALU.pow)
+            return r
+
+        def e_r(eng, t, m):
+            T[("r", t, m)] = rstd(T[("ssum", t, m)], G, "g")
+
+        def e_rs(eng, t, m):
+            s = T[("s", t, m)][:, 0:TCOLS]
+            r = T[("r", t, m)]
+            if eng == "V":
+                nc.vector.tensor_scalar(out=s, in0=s, scalar1=r[:], scalar2=None, op0=ALU.mult)
+            else:
+                nc.scalar.activation(out=s, in_=s, func=ACT.Copy, scale=r[:])
+
+        def e_uo(eng, t):
+            if t == 0:
+                nc.vector.tensor_tensor(out=bso[:], in0=bo1[:], in1=bo2[:], op=ALU.add)
+            uo = work.tile([P, H], F32, name="uo")
+            nc.vector.scalar_tensor_tensor(
+                out=uo[:], in0=T[("s", t, 0)][:, TCOLS:G], scalar=T[("r", t, 0)][:], in1=bso[:], op0=ALU.mult, op1=ALU.add
+            )
+            nc.vector.scalar_tensor_tensor(
+                out=uo[:], in0=T[("s", t, 1)][:, TCOLS:G], scalar=T[("r", t, 1)][:], in1=uo[:], op0=ALU.mult, op1=ALU.add
+            )
+            T[("uo", t)] = uo
+
+        def e_acto(eng, t):
+            og = work.tile([P, H], F32, name="og", bufs=3)
+            nc.scalar.activation(out=og[:], in_=T[("uo", t)][:], func=ACT.Sigmoid)
+            T[("og", t)] = og
+
+        def e_fwd(eng, t, j):
+            zt = ps_tp.tile([P, 4, P], F32, name="tp")
+            for q in range(4):
+                cols = slice((GATE[j] * 4 + q) * P, (GATE[j] * 4 + q + 1) * P)
+                for m in range(2):
+                    nc.tensor.matmul(
+                        out=zt[:, q, :], lhsT=T[("s", t, m)][:, cols], rhs=ident[:], is_transpose=True,
+                        start=(m == 0), stop=(m == 1),
+                    )
+            T[("zt", t, j)] = zt
+
+        def e_act(eng, t, j):
+            gt = work.tile([P, 4, P], F32, name="gate_" + j)
+            for q in range(4):
+                gb = GATE[j] * 4 + q
+                nc.scalar.activation(
+                    out=gt[:, q, :], in_=T[("zt", t, j)][:, q, :], func=(ACT.Tanh if j == "g" else ACT.Sigmoid),
+                    bias=betaT[:, gb:gb + 1], scale=1.0,
+                )
+            T[("gate", t, j)] = gt
+
+        def flat(til):
+            return til[:].rearrange("p q r -> p (q r)")
+
+        def e_cpt(eng, t):
+            cp = ps_tp.tile([P, 4, P], F32, name="tp")
+            view = flat(cp).bitcast(BF16)
+            for q in range(4):
+                nc.tensor.transpose(view[:, q * P:(q + 1) * P], cin[:, t, q * P:(q + 1) * P], identb[:])
+            T[("cpt", t)] = view[:, 0:H]
+
+        def e_q(eng, t):
+            qT = work.tile([P, 4, P], F32, name="qT")
+            nc.vector.tensor_tensor(out=flat(qT), in0=flat(T[("gate", t, "i")]), in1=flat(T[("gate", t, "g")]), op=ALU.mult)
+            T[("qT", t)] = qT
+
+        def e_p(eng, t):
+            pT = work.tile([P, 4, P], F32, name="pT")
+            nc.vector.tensor_tensor(out=flat(pT), in0=flat(T[("gate", t, "f")]), in1=T[("cpt", t)], op=ALU.mult)
+            T[("pT", t)] = pT
+
+        def e_cb(eng, t):
+            cb = ps_tp.tile([P, 4, P], F32, name="tp")
+            for q in range(4):
+                for n, key in enumerate(("pT", "qT")):
+                    nc.tensor.matmul(
+                        out=cb[:, q, :], lhsT=T[(key, t)][:, q, :], rhs=ident[:], is_transpose=True,
+                        start=(n == 0), stop=(n == 1),
+                    )
+            T[("cb", t)] = cb
+
+        def e_ccopy(eng, t):
+            ct = work.tile([P, H], F32, name="ct", bufs=3)
+            csum = small.tile([P, 1], F32, name="csum")
+            nc.scalar.activation(out=ct[:], in_=flat(T[("cb", t)]), func=ACT.Identity, accum_out=csum[:])
+            T[("ct", t)] = ct
+            T[("csum", t)] = csum
+
+        def e_nmc(eng, t):
+            nmc = small.tile([P, 1], F32, name="nmc")
+            if eng == "V":
+                nc.vector.tensor_scalar(out=nmc[:], in0=T[("csum", t)][:], scalar1=-1.0 / H, scalar2=None, op0=ALU.mult)
+            else:
+                nc.scalar.mul(out=nmc[:], in_=T[("csum", t)][:], mul=-1.0 / H)
+            T[("nmc", t)] = nmc
+
+        def e_cstat(eng, t):
+            ssqc = small.tile([P, 1], F32, name="ssqc")
+            nc.scalar.activation(
+                out=junkc[:], in_=T[("ct", t)][:], func=ACT.Square, bias=T[("nmc", t)][:], scale=1.0, accum_out=ssqc[:]
+            )
+            T[("ssqc", t)] = ssqc
+
+        def e_rc(eng, t):
+            T[("rc", t)] = rstd(T[("ssqc", t)], H, "c")
+
+        def e_LN(eng, t):
+            sc = work.tile([P, H], F32, name="sc")
+            nc.vector.scalar_tensor_tensor(
+                out=sc[:], in0=T[("ct", t)][:], scalar=T[("nmc", t)][:], in1=gamc[:], op0=ALU.add, op1=ALU.mult
+            )
+            nc.vector.scalar_tensor_tensor(
+                out=sc[:], in0=sc[:], scalar=T[("rc", t)][:], in1=betc[:], op0=ALU.mult, op1=ALU.add
+            )
+            T[("sc", t)] = sc
+
+        def e_tanh(eng, t):
+            th = work.tile([P, H], F32, name="th")
+            nc.scalar.activation(out=th[:], in_=T[("sc", t)][:], func=ACT.Tanh)
+            T[("th", t)] = th
+
+        def e_h(eng, t):
+            ht = work.tile([P, H], F32, name="ht", bufs=3)
+            nc.vector.tensor_tensor(out=ht[:], in0=T[("og", t)][:], in1=T[("th", t)][:], op=ALU.mult)
+            T[("ht", t)] = ht
+
+        def e_stc(eng, t):
+            nc.sync.dma_start(out=co_v[:, t, :], in_=T[("ct", t)][:])
+
+        def e_sth(eng, t):
+            nc.sync.dma_start(out=ho_v[:, t, :], in_=T[("ht", t)][:])
+
+        tp_drains = ["pre"]
+
+        def tp_slot(drain):
+            tp_drains.append(drain)
+            n = len(tp_drains) - 1
+            return tp_drains[n - TP_BUFS] if n >= TP_BUFS else "pre"
+
+        def unit(t, mk):
+            return 2 * t + mk // 4, mk % 4
+
+        def d_main(t, mk):
+            u, k = unit(t, mk)
+            n = 4 * u + k - ACC_BUFS
+            return "main%d_%d" % (u, k), ["xq%d" % t, "wq%d" % mk, "apply%d_%d" % (n // 4, n % 4)]
+
+        def d_sq(t, mk):
+            u, k = unit(t, mk)
+            deps = ["main%d_%d" % (u, k), "nm%d" % u]
+            if k == 0:
+                deps.extend(["fwd%d_%s" % (t - S_BUFS, j) for j in GATE])
+                deps.append("uo%d" % (t - S_BUFS))
+                deps.append("red%d" % (u - 4))
+            return "sq%d_%d" % (u, k), deps
+
+        def d_apply(t, mk):
+            u, k = unit(t, mk)
+            return "apply%d_%d" % (u, k), ["sq%d_%d" % (u, k)]
+
+        RING = {"f": ("p", 2), "i": ("q", 2), "g": ("q", 2)}
+        STEPS = {
+            "wcopy": (e_wcopy, lambda t, a: ("wcopy%d" % t, ["wq%d" % (t - 4)])),
+            "wq": (e_wq, lambda t, a: ("wq%d" % t, ["wcopy%d" % t])),
+            "ld": (e_ld, lambda t, a: ("ld%d" % (t // GRP), ["xt%d" % (t - GRP - 1)])),
+            "xt": (e_xt, lambda t, a: ("xt%d" % t, ["ld%d" % (t // GRP), tp_slot("xcopy%d" % t)])),
+            "xcopy": (e_xcopy, lambda t, a: ("xcopy%d" % t, ["xt%d" % t, "xq%d" % (t - 2)])),
+            "xq": (e_xq, lambda t, a: ("xq%d" % t, ["xcopy%d" % t, "main%d_3" % (2 * (t - 4) + 1)])),
+            "mean": (e_mean, lambda t, a: ("mean%d" % (2 * t + a), ["xq%d" % t, "wq%d" % (4 * a + 3), "nm%d" % (2 * t + a - 1)])),
+            "nm": (e_nm, lambda t, a: ("nm%d" % (2 * t + a), ["mean%d" % (2 * t + a), "apply%d_3" % (2 * t + a - 4)])),
+            "main": (e_main, d_main),
+            "sq": (e_sq, d_sq),
+            "apply": (e_apply, d_apply),
+            "red": (e_red, lambda t, a: ("red%d" % (2 * t + a), ["sq%d_3" % (2 * t + a), "r%d" % (2 * t + a - 4)])),
+            "r": (e_r, lambda t, a: ("r%d" % (2 * t + a), ["red%d" % (2 * t + a), "rs%d" % (2 * t + a - 4), "uo%d" % (t - 3)])),
+            "rs": (e_rs, lambda t, a: ("rs%d" % (2 * t + a), ["r%d" % (2 * t + a), "apply%d_2" % (2 * t + a)])),
+            "uo": (e_uo, lambda t, a: ("uo%d" % t, ["r%d" % (2 * t), "r%d" % (2 * t + 1), "apply%d_3" % (2 * t), "apply%d_3" % (2 * t + 1), "acto%d" % (t - 2)])),
+            "acto": (e_acto, lambda t, a: ("acto%d" % t, ["uo%d" % t, "h%d" % (t - 3)])),
+            "fwd": (e_fwd, lambda t, a: ("fwd%d_%s" % (t, a), ["rs%d" % (2 * t), "rs%d" % (2 * t + 1), tp_slot("act%d_%s" % (t, a))])),
+            "act": (e_act, lambda t, a: ("act%d_%s" % (t, a), ["fwd%d_%s" % (t, a), "%s%d" % (RING[a][0], t - RING[a][1])])),
+            "cpt": (e_cpt, lambda t, a: ("cpt%d" % t, [tp_slot("p%d" % t)])),
+            "cb": (e_cb, lambda t, a: ("cb%d" % t, ["p%d" % t, "q%d" % t, tp_slot("ccopy%d" % t)])),
+            "q": (e_q, lambda t, a: ("q%d" % t, ["act%d_i" % t, "act%d_g" % t, "cb%d" % (t - 2)])),
+            "p": (e_p, lambda t, a: ("p%d" % t, ["act%d_f" % t, "cpt%d" % t, "cb%d" % (t - 2)])),
+            "ccopy": (e_ccopy, lambda t, a: ("ccopy%d" % t, ["cb%d" % t, "LN%d" % (t - 3), "cstat%d" % (t - 3), "stc%d" % (t - 3)])),
+            "nmc": (e_nmc, lambda t, a: ("nmc%d" % t, ["ccopy%d" % t, "LN%d" % (t - 4)])),
+            "cstat": (e_cstat, lambda t, a: ("cstat%d" % t, ["nmc%d" % t, "rc%d" % (t - 4)])),
+            "rc": (e_rc, lambda t, a: ("rc%d" % t, ["cstat%d" % t, "LN%d" % (t - 4)])),
+            "LN": (e_LN, lambda t, a: ("LN%d" % t, ["rc%d" % t, "tanh%d" % (t - 2)])),
+            "tanh": (e_tanh, lambda t, a: ("tanh%d" % t, ["LN%d" % t, "h%d" % (t - 2)])),
+            "h": (e_h, lambda t, a: ("h%d" % t, ["acto%d" % t, "tanh%d" % t, "sth%d" % (t - 3)])),
+            "stc": (e_stc, lambda t, a: ("stc%d" % t, ["ccopy%d" % t])),
+            "sth": (e_sth, lambda t, a: ("sth%d" % t, ["h%d" % t])),
+        }
+        HEAD = {
+            "PE": (("xt", 0, None), ("xt", 1, None)),
+            "S": (
+                ("xcopy", 0, None), ("xcopy", 1, None), ("wcopy", 1, None), ("wcopy", 3, None), ("wcopy", 5, None),
+                ("wcopy", 7, None),
+            ),
+            "V": (
+                ("xq", 0, None), ("wcopy", 0, None), ("xq", 1, None),
+                ("wcopy", 2, None), ("wq", 0, None), ("wq", 1, None), ("wq", 2, None), ("wcopy", 4, None),
+                ("wq", 3, None), ("wcopy", 6, None), ("wq", 4, None), ("wq", 5, None), ("wq", 6, None), ("wq", 7, None),
+            ),
+            "G": (),
+            "SP": (),
+        }
+
+        queues = {}
+        for eng in ENGINES:
+            todo = list(HEAD[eng])
+            for a in range(-3, NT + 9):
+                for op, off, arg in ORDER[eng]:
+                    t = a + off
+                    if t < 0 or t >= NT:
+                        continue
+                    if op in ("xt", "xcopy", "xq") and t < 2:
+                        continue
+                    if op == "ld" and (t % GRP != 0 or t < 2 * GRP):
+                        continue
+                    todo.append((op, t, arg))
+            queues[eng] = []
+            for op, t, arg in todo:
+                name, deps = STEPS[op][1](t, arg)
+                queues[eng].append((name, deps, op, t, arg))
+
+        names = set()
+        for eng in ENGINES:
+            for item in queues[eng]:
+                names.add(item[0])
+        done = set()
+        at = {eng: 0 for eng in ENGINES}
+        left = len(names)
+        while left > 0:
+            before = left
+            for eng in ENGINES:
+                while at[eng] < len(queues[eng]):
+                    name, deps, op, t, arg = queues[eng][at[eng]]
+                    if any(d in names and d not in done for d in deps):
+                        break
+                    if arg is None:
+                        STEPS[op][0](eng, t)
+                    else:
+                        STEPS[op][0](eng, t, arg)
+                    done.add(name)
+                    at[eng] += 1
+                    left -= 1
+            assert left < before, "the per-engine orders wait for each other"

@@ -249,21 +249,19 @@ def tile_layernormlstmcell_kernel(
 
         def e_red(eng, t, m):
             ssum = small.tile([P, 1], F32, name="ssum")
-            if eng == "V":
-                nc.vector.tensor_reduce(out=ssum[:], in_=T[("ssq", t, m)][:], axis=AX.X, op=ALU.add)
-            else:
-                nc.scalar.activation(out=junkm[:, 0:4], in_=T[("ssq", t, m)][:], func=ACT.Identity, accum_out=ssum[:])
+            nc.scalar.activation(
+                out=junkm[:, 0:4], in_=T[("ssq", t, m)][:], func=ACT.Identity, scale=1.0 / G, bias=EPS / 4,
+                accum_out=ssum[:],
+            )
             T[("ssum", t, m)] = ssum
 
-        def rstd(sumsq, count, nm_):
-            var = small.tile([P, 1], F32, name="var" + nm_)
-            nc.gpsimd.tensor_scalar(out=var[:], in0=sumsq[:], scalar1=1.0 / count, scalar2=EPS, op0=ALU.mult, op1=ALU.add)
+        def rstd(var, nm_):
             r = small.tile([P, 1], F32, name="r" + nm_, bufs=6)
             nc.gpsimd.tensor_tensor(out=r[:], in0=var[:], in1=neghalf[:], op=ALU.pow)
             return r
 
         def e_r(eng, t, m):
-            T[("r", t, m)] = rstd(T[("ssum", t, m)], G, "g")
+            T[("r", t, m)] = rstd(T[("ssum", t, m)], "g")
 
         def e_rs(eng, t, m):
             s = T[("s", t, m)][:, 0:TCOLS]
@@ -361,10 +359,12 @@ def tile_layernormlstmcell_kernel(
             nc.scalar.activation(
                 out=junkc[:], in_=T[("ct", t)][:], func=ACT.Square, bias=T[("nmc", t)][:], scale=1.0, accum_out=ssqc[:]
             )
-            T[("ssqc", t)] = ssqc
+            varc = small.tile([P, 1], F32, name="varc")
+            nc.scalar.activation(out=varc[:], in_=ssqc[:], func=ACT.Identity, scale=1.0 / H, bias=EPS)
+            T[("varc", t)] = varc
 
         def e_rc(eng, t):
-            T[("rc", t)] = rstd(T[("ssqc", t)], H, "c")
+            T[("rc", t)] = rstd(T[("varc", t)], "c")
 
         def e_LN(eng, t):
             sc = work.tile([P, H], F32, name="sc")

@@ -30,8 +30,8 @@ S_BUFS = 3
 
 ORDER = {
     "PE": (
-        ("fwd", -2, "g"), ("main", 0, 6), ("main", 0, 7), ("mean", 1, 0),
-        ("fwd", -2, "f"), ("fwd", -2, "i"), ("main", 1, 0), ("main", 1, 1),
+        ("cor", -2, "g"), ("fwd", -2, "g"), ("main", 0, 6), ("main", 0, 7), ("mean", 1, 0),
+        ("cor", -2, "f"), ("cor", -2, "i"), ("fwd", -2, "f"), ("fwd", -2, "i"), ("main", 1, 0), ("main", 1, 1),
         ("main", 1, 2), ("xt", 2, None), ("main", 1, 3), ("mean", 1, 1),
         ("main", 1, 4), ("cb", -3, None), ("cpt", -2, None), ("main", 1, 5),
     ),
@@ -95,8 +95,12 @@ def tile_layernormlstmcell_kernel(
         gamc = const.tile([P, H], BF16, name="gamc")
         betc = const.tile([P, H], BF16, name="betc")
         cin = const.tile([P, NT, H], BF16, name="cin")
-        bt32 = const.tile([P, P], F32, name="bt32")
-        betaT = const.tile([P, G // P], F32, name="betaT")
+        bet = const.tile([P, 3, P], BF16, name="bet")
+        nc.gpsimd.memset(bet[:], 0.0)
+        sel = const.tile([P, 4, P], BF16, name="sel")
+        nc.gpsimd.memset(sel[:], 0.0)
+        for q in range(4):
+            nc.gpsimd.memset(sel[32 * q:32 * q + 2, q, :], 1.0)
         bso = const.tile([P, H], F32, name="bso")
 
         T = {}
@@ -112,10 +116,10 @@ def tile_layernormlstmcell_kernel(
             first[nm_] = io.tile([P, GRP, K], BF16, name=nm_)
             nc.sync.dma_start(out=first[nm_][:, 0:2, :], in_=view[:, 0:2, :])
             T[(nm_, 0)] = first[nm_]
-        ba = prep.tile([16, P], BF16, name="ba", bufs=1)
-        bb = prep.tile([16, P], BF16, name="bb", bufs=1)
-        nc.scalar.dma_start(out=ba[:], in_=beta_ih.rearrange("(r c) -> r c", c=P))
-        nc.scalar.dma_start(out=bb[:], in_=beta_hh.rearrange("(r c) -> r c", c=P))
+        for v, vec in enumerate((beta_ih, beta_hh)):
+            nc.scalar.dma_start(
+                out=bet[v:P:32, :, :], in_=vec[0:TCOLS].rearrange("(j q c) -> q j c", j=3, q=4)
+            )
         raws = []
         for m, W in enumerate((W_ih, W_hh)):
             for hf in range(2):
@@ -135,12 +139,6 @@ def tile_layernormlstmcell_kernel(
         nc.sync.dma_start(out=bo2[:], in_=beta_hh[TCOLS:G].partition_broadcast(P))
         nc.sync.dma_start(out=gamc[:], in_=gamma_c.partition_broadcast(P))
         nc.sync.dma_start(out=betc[:], in_=beta_c.partition_broadcast(P))
-
-        nc.vector.memset(bt32[:], 0.0)
-        nc.vector.tensor_tensor(out=bt32[0:16, :], in0=ba[:], in1=bb[:], op=ALU.add)
-        tpb = ps_tp.tile([P, 4, P], F32, name="tp")
-        nc.tensor.transpose(tpb[:, 0, :], bt32[:], ident[:])
-        nc.vector.tensor_copy(out=betaT[:], in_=tpb[:, 0, 0:G // P])
 
         def e_wcopy(eng, u):
             grp = prep.tile([P, 512, 4], BF16, name="grp", align_bytes=64)
@@ -288,25 +286,29 @@ def tile_layernormlstmcell_kernel(
             nc.scalar.activation(out=og[:], in_=T[("uo", t)][:], func=ACT.Sigmoid)
             T[("og", t)] = og
 
-        def e_fwd(eng, t, j):
+        def e_cor(eng, t, j):
             zt = ps_tp.tile([P, 4, P], F32, name="tp")
+            nc.tensor.matmul(
+                out=zt[:].rearrange("p q r -> p (q r)"), lhsT=bet[:, GATE[j], :],
+                rhs=sel[:].rearrange("p q r -> p (q r)"), start=True, stop=False,
+            )
+            T[("zt", t, j)] = zt
+
+        def e_fwd(eng, t, j):
+            zt = T[("zt", t, j)]
             for q in range(4):
                 cols = slice((GATE[j] * 4 + q) * P, (GATE[j] * 4 + q + 1) * P)
                 for m in range(2):
                     nc.tensor.matmul(
                         out=zt[:, q, :], lhsT=T[("s", t, m)][:, cols], rhs=ident[:], is_transpose=True,
-                        start=(m == 0), stop=(m == 1),
+                        start=False, stop=(m == 1 and q == 3),
                     )
-            T[("zt", t, j)] = zt
 
         def e_act(eng, t, j):
             gt = work.tile([P, 4, P], F32, name="gate_" + j)
-            for q in range(4):
-                gb = GATE[j] * 4 + q
-                nc.scalar.activation(
-                    out=gt[:, q, :], in_=T[("zt", t, j)][:, q, :], func=(ACT.Tanh if j == "g" else ACT.Sigmoid),
-                    bias=betaT[:, gb:gb + 1], scale=1.0,
-                )
+            nc.scalar.activation(
+                out=flat(gt), in_=flat(T[("zt", t, j)]), func=(ACT.Tanh if j == "g" else ACT.Sigmoid)
+            )
             T[("gate", t, j)] = gt
 
         def flat(til):
@@ -438,7 +440,8 @@ def tile_layernormlstmcell_kernel(
             "rs": (e_rs, lambda t, a: ("rs%d" % (2 * t + a), ["r%d" % (2 * t + a), "apply%d_2" % (2 * t + a)])),
             "uo": (e_uo, lambda t, a: ("uo%d" % t, ["r%d" % (2 * t), "r%d" % (2 * t + 1), "apply%d_3" % (2 * t), "apply%d_3" % (2 * t + 1), "acto%d" % (t - 2)])),
             "acto": (e_acto, lambda t, a: ("acto%d" % t, ["uo%d" % t, "h%d" % (t - 3)])),
-            "fwd": (e_fwd, lambda t, a: ("fwd%d_%s" % (t, a), ["rs%d" % (2 * t), "rs%d" % (2 * t + 1), tp_slot("act%d_%s" % (t, a))])),
+            "cor": (e_cor, lambda t, a: ("cor%d_%s" % (t, a), [tp_slot("act%d_%s" % (t, a))])),
+            "fwd": (e_fwd, lambda t, a: ("fwd%d_%s" % (t, a), ["rs%d" % (2 * t), "rs%d" % (2 * t + 1), "cor%d_%s" % (t, a)])),
             "act": (e_act, lambda t, a: ("act%d_%s" % (t, a), ["fwd%d_%s" % (t, a), "%s%d" % (RING[a][0], t - RING[a][1])])),
             "cpt": (e_cpt, lambda t, a: ("cpt%d" % t, [tp_slot("p%d" % t)])),
             "cb": (e_cb, lambda t, a: ("cb%d" % t, ["p%d" % t, "q%d" % t, tp_slot("ccopy%d" % t)])),

@@ -45,9 +45,9 @@ ORDER = {
     ),
     "V": (
         ("apply", 1, 0), ("apply", 1, 1), ("rs", -1, 1), ("apply", 1, 2),
-        ("apply", 1, 3), ("LN", -5, None), ("xq", 2, None), ("h", -6, None),
-        ("p", -2, None), ("q", -2, None), ("apply", 1, 4), ("apply", 1, 5),
-        ("uo", -1, None), ("apply", 1, 6), ("apply", 1, 7), ("rs", 0, 0),
+        ("apply", 1, 3), ("LN", -5, None), ("xq", 2, None), ("LN2", -5, None), ("h", -6, None),
+        ("p", -2, None), ("q", -2, None), ("apply", 1, 4), ("uo", -1, None), ("apply", 1, 5),
+        ("uo2", -1, None), ("apply", 1, 6), ("apply", 1, 7), ("rs", 0, 0),
     ),
     "G": (
         ("rc", -4, None), ("r", 0, 1), ("r", 1, 0),
@@ -276,10 +276,13 @@ def tile_layernormlstmcell_kernel(
             nc.vector.scalar_tensor_tensor(
                 out=uo[:], in0=T[("s", t, 0)][:, TCOLS:G], scalar=T[("r", t, 0)][:], in1=bso[:], op0=ALU.mult, op1=ALU.add
             )
+            T[("uo", t)] = uo
+
+        def e_uo2(eng, t):
+            uo = T[("uo", t)]
             nc.vector.scalar_tensor_tensor(
                 out=uo[:], in0=T[("s", t, 1)][:, TCOLS:G], scalar=T[("r", t, 1)][:], in1=uo[:], op0=ALU.mult, op1=ALU.add
             )
-            T[("uo", t)] = uo
 
         def e_acto(eng, t):
             og = work.tile([P, H], F32, name="og", bufs=3)
@@ -373,10 +376,13 @@ def tile_layernormlstmcell_kernel(
             nc.vector.scalar_tensor_tensor(
                 out=sc[:], in0=T[("ct", t)][:], scalar=T[("nmc", t)][:], in1=gamc[:], op0=ALU.add, op1=ALU.mult
             )
+            T[("sc", t)] = sc
+
+        def e_LN2(eng, t):
+            sc = T[("sc", t)]
             nc.vector.scalar_tensor_tensor(
                 out=sc[:], in0=sc[:], scalar=T[("rc", t)][:], in1=betc[:], op0=ALU.mult, op1=ALU.add
             )
-            T[("sc", t)] = sc
 
         def e_tanh(eng, t):
             th = work.tile([P, H], F32, name="th")
@@ -414,7 +420,7 @@ def tile_layernormlstmcell_kernel(
             deps = ["main%d_%d" % (u, k), "nm%d" % u]
             if k == 0:
                 deps.extend(["fwd%d_%s" % (t - S_BUFS, j) for j in GATE])
-                deps.append("uo%d" % (t - S_BUFS))
+                deps.append("uo2%d" % (t - S_BUFS))
                 deps.append("red%d" % (u - 4))
             return "sq%d_%d" % (u, k), deps
 
@@ -436,10 +442,12 @@ def tile_layernormlstmcell_kernel(
             "sq": (e_sq, d_sq),
             "apply": (e_apply, d_apply),
             "red": (e_red, lambda t, a: ("red%d" % (2 * t + a), ["sq%d_3" % (2 * t + a), "r%d" % (2 * t + a - 4)])),
-            "r": (e_r, lambda t, a: ("r%d" % (2 * t + a), ["red%d" % (2 * t + a), "rs%d" % (2 * t + a - 4), "uo%d" % (t - 3)])),
+            "r": (e_r, lambda t, a: ("r%d" % (2 * t + a), ["red%d" % (2 * t + a), "rs%d" % (2 * t + a - 4), "uo2%d" % (t - 3)])),
             "rs": (e_rs, lambda t, a: ("rs%d" % (2 * t + a), ["r%d" % (2 * t + a), "apply%d_2" % (2 * t + a)])),
             "uo": (e_uo, lambda t, a: ("uo%d" % t, ["r%d" % (2 * t), "r%d" % (2 * t + 1), "apply%d_3" % (2 * t), "apply%d_3" % (2 * t + 1), "acto%d" % (t - 2)])),
-            "acto": (e_acto, lambda t, a: ("acto%d" % t, ["uo%d" % t, "h%d" % (t - 3)])),
+            "uo2": (e_uo2, lambda t, a: ("uo2%d" % t, ["uo%d" % t])),
+            "LN2": (e_LN2, lambda t, a: ("LN2%d" % t, ["LN%d" % t, "rc%d" % t])),
+            "acto": (e_acto, lambda t, a: ("acto%d" % t, ["uo2%d" % t, "h%d" % (t - 3)])),
             "cor": (e_cor, lambda t, a: ("cor%d_%s" % (t, a), [tp_slot("act%d_%s" % (t, a))])),
             "fwd": (e_fwd, lambda t, a: ("fwd%d_%s" % (t, a), ["rs%d" % (2 * t), "rs%d" % (2 * t + 1), "cor%d_%s" % (t, a)])),
             "act": (e_act, lambda t, a: ("act%d_%s" % (t, a), ["fwd%d_%s" % (t, a), "%s%d" % (RING[a][0], t - RING[a][1])])),
@@ -450,9 +458,9 @@ def tile_layernormlstmcell_kernel(
             "ccopy": (e_ccopy, lambda t, a: ("ccopy%d" % t, ["cb%d" % t, "LN%d" % (t - 3), "cstat%d" % (t - 3), "stc%d" % (t - 3)])),
             "nmc": (e_nmc, lambda t, a: ("nmc%d" % t, ["ccopy%d" % t, "LN%d" % (t - 4)])),
             "cstat": (e_cstat, lambda t, a: ("cstat%d" % t, ["nmc%d" % t, "rc%d" % (t - 4)])),
-            "rc": (e_rc, lambda t, a: ("rc%d" % t, ["cstat%d" % t, "LN%d" % (t - 4)])),
-            "LN": (e_LN, lambda t, a: ("LN%d" % t, ["rc%d" % t, "tanh%d" % (t - 2)])),
-            "tanh": (e_tanh, lambda t, a: ("tanh%d" % t, ["LN%d" % t, "h%d" % (t - 2)])),
+            "rc": (e_rc, lambda t, a: ("rc%d" % t, ["cstat%d" % t, "LN2%d" % (t - 4)])),
+            "LN": (e_LN, lambda t, a: ("LN%d" % t, ["nmc%d" % t, "tanh%d" % (t - 2)])),
+            "tanh": (e_tanh, lambda t, a: ("tanh%d" % t, ["LN2%d" % t, "h%d" % (t - 2)])),
             "h": (e_h, lambda t, a: ("h%d" % t, ["acto%d" % t, "tanh%d" % t, "sth%d" % (t - 3)])),
             "stc": (e_stc, lambda t, a: ("stc%d" % t, ["ccopy%d" % t])),
             "sth": (e_sth, lambda t, a: ("sth%d" % t, ["h%d" % t])),

@@ -30,30 +30,30 @@ S_BUFS = 3
 
 ORDER = {
     "PE": (
-        ("cor", -2, "g"), ("fwd", -2, "g"), ("main", 0, 6), ("main", 0, 7), ("mean", 1, 0),
-        ("cor", -2, "f"), ("cor", -2, "i"), ("fwd", -2, "f"), ("fwd", -2, "i"), ("main", 1, 0), ("main", 1, 1),
+        ("cor", -1, "g"), ("fwd", -1, "g"), ("main", 0, 6), ("main", 0, 7), ("mean", 1, 0),
+        ("cor", -1, "f"), ("cor", -1, "i"), ("fwd", -1, "f"), ("fwd", -1, "i"), ("main", 1, 0), ("main", 1, 1),
         ("main", 1, 2), ("xt", 2, None), ("main", 1, 3), ("mean", 1, 1),
-        ("main", 1, 4), ("cb", -3, None), ("cpt", -2, None), ("main", 1, 5),
+        ("main", 1, 4), ("cb", -2, None), ("cpt", -1, None), ("main", 1, 5),
     ),
     "S": (
-        ("nm", 1, 0), ("sq", 1, 0), ("sq", 1, 1), ("act", -2, "i"),
+        ("sq", 1, 0), ("sq", 1, 1), ("act", -1, "i"),
         ("sq", 1, 2), ("sq", 1, 3), ("xcopy", 2, None), ("nm", 1, 1),
-        ("tanh", -6, None), ("nmc", -4, None), ("red", 0, 0), ("sq", 1, 4),
-        ("sq", 1, 5), ("cstat", -4, None), ("ccopy", -3, None), ("acto", -3, None),
-        ("sq", 1, 6), ("sq", 1, 7), ("act", -1, "g"), ("red", 0, 1),
-        ("act", -1, "f"),
+        ("tanh", -5, None), ("nmc", -3, None), ("red", 1, 0), ("sq", 1, 4),
+        ("sq", 1, 5), ("cstat", -3, None), ("ccopy", -2, None), ("acto", -2, None), ("varc", -3, None),
+        ("sq", 1, 6), ("sq", 1, 7), ("act", 0, "g"), ("red", 1, 1), ("nm", 2, 0),
+        ("act", 0, "f"),
     ),
     "V": (
-        ("apply", 1, 0), ("apply", 1, 1), ("rs", -1, 1), ("apply", 1, 2),
-        ("apply", 1, 3), ("LN", -5, None), ("xq", 2, None), ("LN2", -5, None), ("h", -6, None),
-        ("p", -2, None), ("q", -2, None), ("apply", 1, 4), ("uo", -1, None), ("apply", 1, 5),
-        ("uo2", -1, None), ("apply", 1, 6), ("apply", 1, 7), ("rs", 0, 0),
+        ("apply", 1, 0), ("apply", 1, 1), ("rs", 0, 1), ("apply", 1, 2),
+        ("apply", 1, 3), ("LN", -4, None), ("xq", 2, None), ("LN2", -4, None), ("h", -5, None),
+        ("p", -1, None), ("q", -1, None), ("apply", 1, 4), ("uo", 0, None), ("apply", 1, 5),
+        ("uo2", 0, None), ("apply", 1, 6), ("apply", 1, 7), ("rs", 1, 0),
     ),
     "G": (
-        ("rc", -4, None), ("r", 0, 1), ("r", 1, 0),
+        ("r", 1, 0), ("rc", -3, None), ("r", 1, 1),
     ),
     "SP": (
-        ("ld", 6, None), ("stc", -3, None), ("sth", -6, None),
+        ("ld", 6, None), ("stc", -2, None), ("sth", -5, None),
     ),
 }
 
@@ -111,6 +111,10 @@ def tile_layernormlstmcell_kernel(
                 nc.sync.dma_start(out=til[:], in_=view[:, g * GRP:(g + 1) * GRP, :])
                 T[(nm_, g)] = til
 
+        raws = {}
+        for u in range(2):
+            raws[u] = prep.tile([P, 4, 512], BF16, name="raw0", bufs=2)
+        nc.sync.dma_start(out=raws[0][:], in_=W_ih[:, 0:512].rearrange("(p e) c -> p e c", e=4))
         first = {}
         for nm_, view in (("xin", x_v), ("hin", h_v)):
             first[nm_] = io.tile([P, GRP, K], BF16, name=nm_)
@@ -120,14 +124,18 @@ def tile_layernormlstmcell_kernel(
             nc.scalar.dma_start(
                 out=bet[v:P:32, :, :], in_=vec[0:TCOLS].rearrange("(j q c) -> q j c", j=3, q=4)
             )
-        raws = []
+        nc.sync.dma_start(out=raws[1][:], in_=W_ih[:, 512:1024].rearrange("(p e) c -> p e c", e=4))
         for m, W in enumerate((W_ih, W_hh)):
             for hf in range(2):
-                raw = prep.tile([P, 4, 1024], BF16, name="raw")
+                if m == 0 and hf == 0:
+                    continue
+                raw = prep.tile([P, 4, 1024], BF16, name="raw", bufs=3)
                 nc.sync.dma_start(
                     out=raw[:], in_=W[:, hf * 1024:(hf + 1) * 1024].rearrange("(p e) c -> p e c", e=4)
                 )
-                raws.append(raw)
+                for n in range(2):
+                    raws[4 * m + 2 * hf + n] = raw[:, :, n * 512:(n + 1) * 512]
+        for m in range(2):
             nc.sync.dma_start(out=gam[m][:], in_=(gamma_ih, gamma_hh)[m].partition_broadcast(P))
         for nm_, view in (("xin", x_v), ("hin", h_v)):
             nc.sync.dma_start(out=first[nm_][:, 2:GRP, :], in_=view[:, 2:GRP, :])
@@ -143,7 +151,7 @@ def tile_layernormlstmcell_kernel(
         def e_wcopy(eng, u):
             grp = prep.tile([P, 512, 4], BF16, name="grp", align_bytes=64)
             dst = grp[:].rearrange("p (c i) t -> p c t i", i=4)
-            src = raws[u // 2][:, :, (u % 2) * 512:(u % 2 + 1) * 512].rearrange("p t (c i) -> p c t i", i=4)
+            src = (raws[u][:] if u < 2 else raws[u]).rearrange("p t (c i) -> p c t i", i=4)
             if eng == "V":
                 nc.vector.tensor_copy(out=dst, in_=src)
             else:
@@ -272,7 +280,7 @@ def tile_layernormlstmcell_kernel(
         def e_uo(eng, t):
             if t == 0:
                 nc.vector.tensor_tensor(out=bso[:], in0=bo1[:], in1=bo2[:], op=ALU.add)
-            uo = work.tile([P, H], F32, name="uo")
+            uo = work.tile([P, H], F32, name="uo", bufs=3)
             nc.vector.scalar_tensor_tensor(
                 out=uo[:], in0=T[("s", t, 0)][:, TCOLS:G], scalar=T[("r", t, 0)][:], in1=bso[:], op0=ALU.mult, op1=ALU.add
             )
@@ -364,6 +372,10 @@ def tile_layernormlstmcell_kernel(
             nc.scalar.activation(
                 out=junkc[:], in_=T[("ct", t)][:], func=ACT.Square, bias=T[("nmc", t)][:], scale=1.0, accum_out=ssqc[:]
             )
+            T[("ssqc", t)] = ssqc
+
+        def e_varc(eng, t):
+            ssqc = T[("ssqc", t)]
             varc = small.tile([P, 1], F32, name="varc")
             nc.scalar.activation(out=varc[:], in_=ssqc[:], func=ACT.Identity, scale=1.0 / H, bias=EPS)
             T[("varc", t)] = varc
@@ -444,7 +456,7 @@ def tile_layernormlstmcell_kernel(
             "red": (e_red, lambda t, a: ("red%d" % (2 * t + a), ["sq%d_3" % (2 * t + a), "r%d" % (2 * t + a - 4)])),
             "r": (e_r, lambda t, a: ("r%d" % (2 * t + a), ["red%d" % (2 * t + a), "rs%d" % (2 * t + a - 4), "uo2%d" % (t - 3)])),
             "rs": (e_rs, lambda t, a: ("rs%d" % (2 * t + a), ["r%d" % (2 * t + a), "apply%d_2" % (2 * t + a)])),
-            "uo": (e_uo, lambda t, a: ("uo%d" % t, ["r%d" % (2 * t), "r%d" % (2 * t + 1), "apply%d_3" % (2 * t), "apply%d_3" % (2 * t + 1), "acto%d" % (t - 2)])),
+            "uo": (e_uo, lambda t, a: ("uo%d" % t, ["r%d" % (2 * t), "r%d" % (2 * t + 1), "apply%d_3" % (2 * t), "apply%d_3" % (2 * t + 1), "acto%d" % (t - 3)])),
             "uo2": (e_uo2, lambda t, a: ("uo2%d" % t, ["uo%d" % t])),
             "LN2": (e_LN2, lambda t, a: ("LN2%d" % t, ["LN%d" % t, "rc%d" % t])),
             "acto": (e_acto, lambda t, a: ("acto%d" % t, ["uo2%d" % t, "h%d" % (t - 3)])),
@@ -458,7 +470,8 @@ def tile_layernormlstmcell_kernel(
             "ccopy": (e_ccopy, lambda t, a: ("ccopy%d" % t, ["cb%d" % t, "LN%d" % (t - 3), "cstat%d" % (t - 3), "stc%d" % (t - 3)])),
             "nmc": (e_nmc, lambda t, a: ("nmc%d" % t, ["ccopy%d" % t, "LN%d" % (t - 4)])),
             "cstat": (e_cstat, lambda t, a: ("cstat%d" % t, ["nmc%d" % t, "rc%d" % (t - 4)])),
-            "rc": (e_rc, lambda t, a: ("rc%d" % t, ["cstat%d" % t, "LN2%d" % (t - 4)])),
+            "varc": (e_varc, lambda t, a: ("varc%d" % t, ["cstat%d" % t, "rc%d" % (t - 4)])),
+            "rc": (e_rc, lambda t, a: ("rc%d" % t, ["varc%d" % t, "LN2%d" % (t - 4)])),
             "LN": (e_LN, lambda t, a: ("LN%d" % t, ["nmc%d" % t, "tanh%d" % (t - 2)])),
             "tanh": (e_tanh, lambda t, a: ("tanh%d" % t, ["LN2%d" % t, "h%d" % (t - 2)])),
             "h": (e_h, lambda t, a: ("h%d" % t, ["acto%d" % t, "tanh%d" % t, "sth%d" % (t - 3)])),
@@ -468,13 +481,12 @@ def tile_layernormlstmcell_kernel(
         HEAD = {
             "PE": (("xt", 0, None), ("xt", 1, None)),
             "S": (
-                ("xcopy", 0, None), ("xcopy", 1, None), ("wcopy", 1, None), ("wcopy", 3, None), ("wcopy", 5, None),
-                ("wcopy", 7, None),
+                ("xcopy", 0, None), ("wcopy", 1, None), ("xcopy", 1, None), ("wcopy", 3, None), ("wcopy", 5, None),
             ),
             "V": (
-                ("xq", 0, None), ("wcopy", 0, None), ("xq", 1, None),
-                ("wcopy", 2, None), ("wq", 0, None), ("wq", 1, None), ("wq", 2, None), ("wcopy", 4, None),
-                ("wq", 3, None), ("wcopy", 6, None), ("wq", 4, None), ("wq", 5, None), ("wq", 6, None), ("wq", 7, None),
+                ("wcopy", 0, None), ("xq", 0, None), ("wq", 0, None), ("wcopy", 2, None), ("wq", 1, None),
+                ("xq", 1, None), ("wq", 2, None), ("wcopy", 4, None), ("wq", 3, None),
+                ("wq", 4, None), ("wcopy", 6, None), ("wq", 5, None), ("wcopy", 7, None), ("wq", 6, None), ("wq", 7, None),
             ),
             "G": (),
             "SP": (),

@@ -30,10 +30,10 @@ S_BUFS = 3
 
 ORDER = {
     "PE": (
-        ("cor", -1, "g"), ("fwd", -1, "g"), ("main", 0, 6), ("main", 0, 7), ("mean", 1, 0),
+        ("main", 0, 6), ("main", 0, 7), ("mean", 1, 0),
         ("cor", -1, "f"), ("cor", -1, "i"), ("fwd", -1, "f"), ("fwd", -1, "i"), ("main", 1, 0), ("main", 1, 1),
         ("main", 1, 2), ("xt", 2, None), ("main", 1, 3), ("mean", 1, 1),
-        ("main", 1, 4), ("cb", -2, None), ("cpt", -1, None), ("main", 1, 5),
+        ("main", 1, 4), ("main", 1, 5), ("cb", -2, None), ("cpt", -1, None), ("cor", 0, "g"), ("fwd", 0, "g"),
     ),
     "S": (
         ("sq", 1, 0), ("sq", 1, 1), ("act", -1, "i"),
@@ -87,6 +87,7 @@ def tile_layernormlstmcell_kernel(
         identb = const.tile([P, P], BF16, name="identb")
         nc.vector.tensor_copy(out=identb[:], in_=ident[:])
         junkm = const.tile([P, P], F32, name="junkm")
+        junkr = const.tile([P, 8], F32, name="junkr")
         junkv = const.tile([P, P], F32, name="junkv")
         junkc = const.tile([P, H], F32, name="junkc")
         wc = [const.tile([P, G], U32, name="wc%d" % m, align_bytes=64) for m in range(2)]
@@ -256,7 +257,7 @@ def tile_layernormlstmcell_kernel(
         def e_red(eng, t, m):
             ssum = small.tile([P, 1], F32, name="ssum")
             nc.scalar.activation(
-                out=junkm[:, 0:4], in_=T[("ssq", t, m)][:], func=ACT.Identity, scale=1.0 / G, bias=EPS / 4,
+                out=junkr[:, 4 * m:4 * m + 4], in_=T[("ssq", t, m)][:], func=ACT.Identity, scale=1.0 / G, bias=EPS / 4,
                 accum_out=ssum[:],
             )
             T[("ssum", t, m)] = ssum

@@ -30,27 +30,25 @@ S_BUFS = 3
 
 ORDER = {
     "PE": (
-        ("main", 0, 6), ("main", 0, 7), ("mean", 1, 0),
-        ("cor", -1, "f"), ("cor", -1, "i"), ("fwd", -1, "f"), ("fwd", -1, "i"), ("main", 1, 0), ("main", 1, 1),
-        ("main", 1, 2), ("xt", 2, None), ("main", 1, 3), ("mean", 1, 1),
-        ("main", 1, 4), ("main", 1, 5), ("cb", -2, None), ("cpt", -1, None), ("cor", 0, "g"), ("fwd", 0, "g"),
+        ("main", 0, 2), ("main", 0, 3), ("xt", 2, None), ("mean", 1, 0), ("mean", 1, 1),
+        ("main", 0, 4), ("main", 0, 5), ("fwd", -1, "f"), ("mean", 1, 2), ("mean", 1, 3),
+        ("main", 0, 6), ("main", 0, 7), ("fwd", -1, "i"), ("cb", -2, None), ("mean", 1, 4), ("mean", 1, 5),
+        ("main", 1, 0), ("main", 1, 1), ("fwd", -1, "g"), ("cpt", -1, None), ("mean", 1, 6), ("mean", 1, 7),
     ),
     "S": (
-        ("sq", 1, 0), ("sq", 1, 1), ("act", -1, "i"),
-        ("sq", 1, 2), ("sq", 1, 3), ("xcopy", 2, None), ("nm", 1, 1),
-        ("tanh", -5, None), ("nmc", -3, None), ("red", 1, 0), ("sq", 1, 4),
-        ("sq", 1, 5), ("cstat", -3, None), ("ccopy", -2, None), ("acto", -2, None), ("varc", -3, None),
-        ("sq", 1, 6), ("sq", 1, 7), ("act", 0, "g"), ("red", 1, 1), ("nm", 2, 0),
-        ("act", 0, "f"),
+        ("sq", 0, 0), ("sq", 0, 1), ("nm", 0, 1), ("act", -2, "g"), ("nmc", -3, None), ("tanh", -5, None),
+        ("sq", 0, 2), ("sq", 0, 3), ("red", 0, 0), ("xcopy", 2, None), ("cstat", -3, None),
+        ("sq", 0, 4), ("sq", 0, 5), ("nm", 1, 0), ("act", -1, "f"), ("varc", -3, None), ("acto", -1, None),
+        ("sq", 0, 6), ("sq", 0, 7), ("red", 0, 1), ("act", -1, "i"), ("ccopy", -2, None),
     ),
     "V": (
-        ("apply", 1, 0), ("apply", 1, 1), ("rs", 0, 1), ("apply", 1, 2),
-        ("apply", 1, 3), ("LN", -4, None), ("xq", 2, None), ("LN2", -4, None), ("h", -5, None),
-        ("p", -1, None), ("q", -1, None), ("apply", 1, 4), ("uo", 0, None), ("apply", 1, 5),
-        ("uo2", 0, None), ("apply", 1, 6), ("apply", 1, 7), ("rs", 1, 0),
+        ("apply", 0, 0), ("apply", 0, 1), ("rs", -1, 1), ("p", -2, None),
+        ("apply", 0, 2), ("apply", 0, 3), ("q", -2, None), ("uo2", -1, None), ("LN2", -4, None),
+        ("apply", 0, 4), ("apply", 0, 5), ("xq", 2, None), ("rs", 0, 0), ("h", -5, None),
+        ("apply", 0, 6), ("apply", 0, 7), ("uo", 0, None), ("LN", -3, None),
     ),
     "G": (
-        ("r", 1, 0), ("rc", -3, None), ("r", 1, 1),
+        ("r", 0, 0), ("rc", -3, None), ("r", 0, 1),
     ),
     "SP": (
         ("ld", 6, None), ("stc", -2, None), ("sth", -5, None),
@@ -96,12 +94,9 @@ def tile_layernormlstmcell_kernel(
         gamc = const.tile([P, H], BF16, name="gamc")
         betc = const.tile([P, H], BF16, name="betc")
         cin = const.tile([P, NT, H], BF16, name="cin")
-        bet = const.tile([P, 3, P], BF16, name="bet")
-        nc.gpsimd.memset(bet[:], 0.0)
-        sel = const.tile([P, 4, P], BF16, name="sel")
-        nc.gpsimd.memset(sel[:], 0.0)
-        for q in range(4):
-            nc.gpsimd.memset(sel[32 * q:32 * q + 2, q, :], 1.0)
+        brow = const.tile([P, P], BF16, name="brow")
+        nc.gpsimd.memset(brow[:], 0.0)
+        bet = const.tile([P, 12], F32, name="bet")
         bso = const.tile([P, H], F32, name="bso")
 
         T = {}
@@ -121,10 +116,6 @@ def tile_layernormlstmcell_kernel(
             first[nm_] = io.tile([P, GRP, K], BF16, name=nm_)
             nc.sync.dma_start(out=first[nm_][:, 0:2, :], in_=view[:, 0:2, :])
             T[(nm_, 0)] = first[nm_]
-        for v, vec in enumerate((beta_ih, beta_hh)):
-            nc.scalar.dma_start(
-                out=bet[v:P:32, :, :], in_=vec[0:TCOLS].rearrange("(j q c) -> q j c", j=3, q=4)
-            )
         nc.sync.dma_start(out=raws[1][:], in_=W_ih[:, 512:1024].rearrange("(p e) c -> p e c", e=4))
         for m, W in enumerate((W_ih, W_hh)):
             for hf in range(2):
@@ -136,16 +127,18 @@ def tile_layernormlstmcell_kernel(
                 )
                 for n in range(2):
                     raws[4 * m + 2 * hf + n] = raw[:, :, n * 512:(n + 1) * 512]
+        for v, vec in enumerate((beta_ih, beta_hh)):
+            nc.sync.dma_start(out=brow[12 * v:12 * v + 12, :], in_=vec[0:TCOLS].rearrange("(b c) -> b c", c=P))
         for m in range(2):
             nc.sync.dma_start(out=gam[m][:], in_=(gamma_ih, gamma_hh)[m].partition_broadcast(P))
-        for nm_, view in (("xin", x_v), ("hin", h_v)):
-            nc.sync.dma_start(out=first[nm_][:, 2:GRP, :], in_=view[:, 2:GRP, :])
-        nc.sync.dma_start(out=cin[:], in_=c_v)
-        load_group(1)
         bo1 = prep.tile([P, H], BF16, name="bo1", bufs=1)
         bo2 = prep.tile([P, H], BF16, name="bo2", bufs=1)
         nc.sync.dma_start(out=bo1[:], in_=beta_ih[TCOLS:G].partition_broadcast(P))
         nc.sync.dma_start(out=bo2[:], in_=beta_hh[TCOLS:G].partition_broadcast(P))
+        for nm_, view in (("xin", x_v), ("hin", h_v)):
+            nc.sync.dma_start(out=first[nm_][:, 2:GRP, :], in_=view[:, 2:GRP, :])
+        nc.sync.dma_start(out=cin[:], in_=c_v)
+        load_group(1)
         nc.sync.dma_start(out=gamc[:], in_=gamma_c.partition_broadcast(P))
         nc.sync.dma_start(out=betc[:], in_=beta_c.partition_broadcast(P))
 
@@ -158,6 +151,25 @@ def tile_layernormlstmcell_kernel(
             else:
                 nc.scalar.copy(out=dst, in_=src)
             T[("grp", u)] = grp
+
+        def e_wt(eng, u, half):
+            wt = ps_tp.tile([P, 4, P], F32, name="tp")
+            view = flat(wt).bitcast(BF16)
+            src = raws[u][:] if u < 2 else raws[u]
+            for n in range(2):
+                c0 = (2 * half + n) * P
+                nc.tensor.matmul(
+                    out=view[:, n * 512:(n + 1) * 512], lhsT=identb[:],
+                    rhs=src[:, :, c0:c0 + P].rearrange("p t c -> p c t"), start=True, stop=True,
+                )
+            T[("wt", u, half)] = view
+
+        def e_wtc(eng, u, half):
+            if half == 0:
+                T[("grp", u)] = prep.tile([P, 512, 4], BF16, name="grp", align_bytes=64)
+            nc.scalar.copy(
+                out=T[("grp", u)][:, half * 256:half * 256 + 256, :].rearrange("p c t -> p (c t)"), in_=T[("wt", u, half)]
+            )
 
         def e_wq(eng, u):
             m = u // 4
@@ -211,11 +223,12 @@ def tile_layernormlstmcell_kernel(
                 stop=stop,
             )
 
-        def e_mean(eng, t, m):
-            mp = ps_mean.tile([P, P], F32, name="mean_ps")
-            for j in range(G // P):
-                mx(mp[:], t, m, slice(j * P, (j + 1) * P), j == 0, j == G // P - 1)
-            T[("mean", t, m)] = mp
+        def e_mean(eng, t, mk):
+            m, k = mk // 4, mk % 4
+            if k == 0:
+                T[("mean", t, m)] = ps_mean.tile([P, P], F32, name="mean_ps")
+            for j in range(4 * k, 4 * k + 4):
+                mx(T[("mean", t, m)][:], t, m, slice(j * P, (j + 1) * P), j == 0, j == G // P - 1)
 
         def e_nm(eng, t, m):
             nm = small.tile([P, 1], F32, name="nm")
@@ -294,33 +307,40 @@ def tile_layernormlstmcell_kernel(
             )
 
         def e_acto(eng, t):
-            og = work.tile([P, H], F32, name="og", bufs=3)
+            og = work.tile([P, H], F32, name="og", bufs=5)
             nc.scalar.activation(out=og[:], in_=T[("uo", t)][:], func=ACT.Sigmoid)
             T[("og", t)] = og
 
-        def e_cor(eng, t, j):
-            zt = ps_tp.tile([P, 4, P], F32, name="tp")
-            nc.tensor.matmul(
-                out=zt[:].rearrange("p q r -> p (q r)"), lhsT=bet[:, GATE[j], :],
-                rhs=sel[:].rearrange("p q r -> p (q r)"), start=True, stop=False,
-            )
-            T[("zt", t, j)] = zt
+        def e_bt(eng, t):
+            cols = ps_tp.tile([P, 4, P], F32, name="tp")
+            view = flat(cols).bitcast(BF16)
+            nc.tensor.transpose(view[:, 0:P], brow[:], identb[:])
+            T["bcols"] = view
+
+        def e_bcopy(eng, t):
+            half = small.tile([P, 12], F32, name="half")
+            nc.vector.tensor_copy(out=half[:], in_=T["bcols"][:, 0:12])
+            nc.vector.tensor_tensor(out=bet[:], in0=half[:], in1=T["bcols"][:, 12:24], op=ALU.add)
 
         def e_fwd(eng, t, j):
-            zt = T[("zt", t, j)]
+            zt = ps_tp.tile([P, 4, P], F32, name="tp")
+            T[("zt", t, j)] = zt
             for q in range(4):
                 cols = slice((GATE[j] * 4 + q) * P, (GATE[j] * 4 + q + 1) * P)
                 for m in range(2):
                     nc.tensor.matmul(
                         out=zt[:, q, :], lhsT=T[("s", t, m)][:, cols], rhs=ident[:], is_transpose=True,
-                        start=False, stop=(m == 1 and q == 3),
+                        start=(m == 0), stop=(m == 1),
                     )
 
         def e_act(eng, t, j):
             gt = work.tile([P, 4, P], F32, name="gate_" + j)
-            nc.scalar.activation(
-                out=flat(gt), in_=flat(T[("zt", t, j)]), func=(ACT.Tanh if j == "g" else ACT.Sigmoid)
-            )
+            for q in range(4):
+                b = GATE[j] * 4 + q
+                nc.scalar.activation(
+                    out=gt[:, q, :], in_=T[("zt", t, j)][:, q, :], func=(ACT.Tanh if j == "g" else ACT.Sigmoid),
+                    bias=bet[:, b:b + 1],
+                )
             T[("gate", t, j)] = gt
 
         def flat(til):
@@ -444,26 +464,29 @@ def tile_layernormlstmcell_kernel(
         RING = {"f": ("p", 2), "i": ("q", 2), "g": ("q", 2)}
         STEPS = {
             "wcopy": (e_wcopy, lambda t, a: ("wcopy%d" % t, ["wq%d" % (t - 4)])),
-            "wq": (e_wq, lambda t, a: ("wq%d" % t, ["wcopy%d" % t])),
+            "wt": (e_wt, lambda t, a: ("wt%d_%d" % (t, a), [tp_slot("wtc%d_%d" % (t, a))])),
+            "wtc": (e_wtc, lambda t, a: ("wtc%d_%d" % (t, a), ["wt%d_%d" % (t, a), "wq%d" % (t - 3)])),
+            "wq": (e_wq, lambda t, a: ("wq%d" % t, ["wcopy%d" % t, "wtc%d_1" % t])),
             "ld": (e_ld, lambda t, a: ("ld%d" % (t // GRP), ["xt%d" % (t - GRP - 1)])),
             "xt": (e_xt, lambda t, a: ("xt%d" % t, ["ld%d" % (t // GRP), tp_slot("xcopy%d" % t)])),
             "xcopy": (e_xcopy, lambda t, a: ("xcopy%d" % t, ["xt%d" % t, "xq%d" % (t - 2)])),
             "xq": (e_xq, lambda t, a: ("xq%d" % t, ["xcopy%d" % t, "main%d_3" % (2 * (t - 4) + 1)])),
-            "mean": (e_mean, lambda t, a: ("mean%d" % (2 * t + a), ["xq%d" % t, "wq%d" % (4 * a + 3), "nm%d" % (2 * t + a - 1)])),
-            "nm": (e_nm, lambda t, a: ("nm%d" % (2 * t + a), ["mean%d" % (2 * t + a), "apply%d_3" % (2 * t + a - 4)])),
+            "mean": (e_mean, lambda t, a: ("mean%d_%d" % unit(t, a), ["xq%d" % t, "wq%d" % a] + (["nm%d" % (unit(t, a)[0] - 1)] if a % 4 == 0 else []))),
+            "nm": (e_nm, lambda t, a: ("nm%d" % (2 * t + a), ["mean%d_3" % (2 * t + a), "apply%d_3" % (2 * t + a - 4)])),
             "main": (e_main, d_main),
             "sq": (e_sq, d_sq),
             "apply": (e_apply, d_apply),
             "red": (e_red, lambda t, a: ("red%d" % (2 * t + a), ["sq%d_3" % (2 * t + a), "r%d" % (2 * t + a - 4)])),
             "r": (e_r, lambda t, a: ("r%d" % (2 * t + a), ["red%d" % (2 * t + a), "rs%d" % (2 * t + a - 4), "uo2%d" % (t - 3)])),
             "rs": (e_rs, lambda t, a: ("rs%d" % (2 * t + a), ["r%d" % (2 * t + a), "apply%d_2" % (2 * t + a)])),
-            "uo": (e_uo, lambda t, a: ("uo%d" % t, ["r%d" % (2 * t), "r%d" % (2 * t + 1), "apply%d_3" % (2 * t), "apply%d_3" % (2 * t + 1), "acto%d" % (t - 3)])),
-            "uo2": (e_uo2, lambda t, a: ("uo2%d" % t, ["uo%d" % t])),
+            "uo": (e_uo, lambda t, a: ("uo%d" % t, ["r%d" % (2 * t), "apply%d_3" % (2 * t), "acto%d" % (t - 3)])),
+            "uo2": (e_uo2, lambda t, a: ("uo2%d" % t, ["uo%d" % t, "r%d" % (2 * t + 1), "apply%d_3" % (2 * t + 1)])),
             "LN2": (e_LN2, lambda t, a: ("LN2%d" % t, ["LN%d" % t, "rc%d" % t])),
-            "acto": (e_acto, lambda t, a: ("acto%d" % t, ["uo2%d" % t, "h%d" % (t - 3)])),
-            "cor": (e_cor, lambda t, a: ("cor%d_%s" % (t, a), [tp_slot("act%d_%s" % (t, a))])),
-            "fwd": (e_fwd, lambda t, a: ("fwd%d_%s" % (t, a), ["rs%d" % (2 * t), "rs%d" % (2 * t + 1), "cor%d_%s" % (t, a)])),
-            "act": (e_act, lambda t, a: ("act%d_%s" % (t, a), ["fwd%d_%s" % (t, a), "%s%d" % (RING[a][0], t - RING[a][1])])),
+            "acto": (e_acto, lambda t, a: ("acto%d" % t, ["uo2%d" % t, "h%d" % (t - 5)])),
+            "bt": (e_bt, lambda t, a: ("bt0", [tp_slot("bcopy0")])),
+            "bcopy": (e_bcopy, lambda t, a: ("bcopy0", ["bt0"])),
+            "fwd": (e_fwd, lambda t, a: ("fwd%d_%s" % (t, a), ["rs%d" % (2 * t), "rs%d" % (2 * t + 1), tp_slot("act%d_%s" % (t, a))])),
+            "act": (e_act, lambda t, a: ("act%d_%s" % (t, a), ["bcopy0", "fwd%d_%s" % (t, a), "%s%d" % (RING[a][0], t - RING[a][1])])),
             "cpt": (e_cpt, lambda t, a: ("cpt%d" % t, [tp_slot("p%d" % t)])),
             "cb": (e_cb, lambda t, a: ("cb%d" % t, ["p%d" % t, "q%d" % t, tp_slot("ccopy%d" % t)])),
             "q": (e_q, lambda t, a: ("q%d" % t, ["act%d_i" % t, "act%d_g" % t, "cb%d" % (t - 2)])),
@@ -480,14 +503,18 @@ def tile_layernormlstmcell_kernel(
             "sth": (e_sth, lambda t, a: ("sth%d" % t, ["h%d" % t])),
         }
         HEAD = {
-            "PE": (("xt", 0, None), ("xt", 1, None)),
+            "PE": (
+                ("xt", 0, None), ("wt", 1, 0), ("wt", 1, 1), ("xt", 1, None), ("wt", 3, 0), ("wt", 3, 1),
+                ("wt", 5, 0), ("wt", 5, 1), ("wt", 6, 0), ("wt", 6, 1), ("bt", 0, None),
+            ),
             "S": (
-                ("xcopy", 0, None), ("wcopy", 1, None), ("xcopy", 1, None), ("wcopy", 3, None), ("wcopy", 5, None),
+                ("xcopy", 0, None), ("wtc", 1, 0), ("wtc", 1, 1), ("xcopy", 1, None), ("wtc", 3, 0), ("wtc", 3, 1),
+                ("wtc", 5, 0), ("wtc", 5, 1), ("wtc", 6, 0), ("wtc", 6, 1),
             ),
             "V": (
                 ("wcopy", 0, None), ("xq", 0, None), ("wq", 0, None), ("wcopy", 2, None), ("wq", 1, None),
                 ("xq", 1, None), ("wq", 2, None), ("wcopy", 4, None), ("wq", 3, None),
-                ("wq", 4, None), ("wcopy", 6, None), ("wq", 5, None), ("wcopy", 7, None), ("wq", 6, None), ("wq", 7, None),
+                ("wq", 4, None), ("wq", 5, None), ("wcopy", 7, None), ("wq", 6, None), ("wq", 7, None), ("bcopy", 0, None),
             ),
             "G": (),
             "SP": (),

@@ -30,25 +30,26 @@ S_BUFS = 3
 
 ORDER = {
     "PE": (
-        ("main", 0, 2), ("main", 0, 3), ("xt", 2, None), ("mean", 1, 0), ("mean", 1, 1),
-        ("main", 0, 4), ("main", 0, 5), ("fwd", -1, "f"), ("mean", 1, 2), ("mean", 1, 3),
-        ("main", 0, 6), ("main", 0, 7), ("fwd", -1, "i"), ("cb", -2, None), ("mean", 1, 4), ("mean", 1, 5),
-        ("main", 1, 0), ("main", 1, 1), ("fwd", -1, "g"), ("cpt", -1, None), ("mean", 1, 6), ("mean", 1, 7),
+        ("xt", 2, None), ("fwd", -2, "g"), ("cpt", -2, None),
+        ("mean", 1, 0), ("main", 0, 4), ("mean", 1, 1), ("main", 0, 5), ("mean", 1, 2), ("main", 0, 6), ("mean", 1, 3), ("main", 0, 7),
+        ("fwd", -1, "f"),
+        ("mean", 1, 4), ("mean", 1, 5), ("mean", 1, 6),
+        ("fwd", -1, "i"), ("cb", -2, None),
+        ("mean", 1, 7), ("main", 1, 0), ("main", 1, 1), ("main", 1, 2), ("main", 1, 3),
     ),
     "S": (
-        ("sq", 0, 0), ("sq", 0, 1), ("nm", 0, 1), ("act", -2, "g"), ("nmc", -3, None), ("tanh", -5, None),
-        ("sq", 0, 2), ("sq", 0, 3), ("red", 0, 0), ("xcopy", 2, None), ("cstat", -3, None),
-        ("sq", 0, 4), ("sq", 0, 5), ("nm", 1, 0), ("act", -1, "f"), ("varc", -3, None), ("acto", -1, None),
-        ("sq", 0, 6), ("sq", 0, 7), ("red", 0, 1), ("act", -1, "i"), ("ccopy", -2, None),
+        ("sq", 0, 0), ("sq", 0, 1), ("sq", 0, 2), ("sq", 0, 3), ("nmc", -3, None), ("act", -2, "g"), ("red", 0, 0), ("cstat", -3, None),
+        ("sq", 0, 4), ("sq", 0, 5), ("nm", 1, 0), ("sq", 0, 6), ("acto", -2, None), ("sq", 0, 7), ("varc", -3, None),
+        ("act", -1, "f"), ("red", 0, 1), ("act", -1, "i"), ("ccopy", -2, None), ("nm", 1, 1), ("tanh", -4, None),
     ),
     "V": (
-        ("apply", 0, 0), ("apply", 0, 1), ("rs", -1, 1), ("p", -2, None),
-        ("apply", 0, 2), ("apply", 0, 3), ("q", -2, None), ("uo2", -1, None), ("LN2", -4, None),
-        ("apply", 0, 4), ("apply", 0, 5), ("xq", 2, None), ("rs", 0, 0), ("h", -5, None),
-        ("apply", 0, 6), ("apply", 0, 7), ("uo", 0, None), ("LN", -3, None),
+        ("apply", 0, 0), ("apply", 0, 1), ("xcopy", 2, None), ("apply", 0, 2), ("apply", 0, 3),
+        ("rs", -1, 1), ("xq", 2, None), ("p", -2, None), ("uo2", -1, None), ("q", -2, None),
+        ("apply", 0, 4), ("apply", 0, 5), ("apply", 0, 6), ("apply", 0, 7),
+        ("LN2", -4, None), ("h", -5, None), ("uo", 0, None), ("rs", 0, 0), ("LN", -3, None),
     ),
     "G": (
-        ("r", 0, 0), ("rc", -3, None), ("r", 0, 1),
+        ("h", -5, None), ("r", -1, 1), ("q", -2, None), ("r", 0, 0), ("rc", -3, None),
     ),
     "SP": (
         ("ld", 6, None), ("stc", -2, None), ("sth", -5, None),
@@ -353,9 +354,12 @@ def tile_layernormlstmcell_kernel(
                 nc.tensor.transpose(view[:, q * P:(q + 1) * P], cin[:, t, q * P:(q + 1) * P], identb[:])
             T[("cpt", t)] = view[:, 0:H]
 
+        def product(eng):
+            return nc.vector.tensor_tensor if eng == "V" else nc.gpsimd.tensor_tensor
+
         def e_q(eng, t):
-            qT = work.tile([P, 4, P], F32, name="qT")
-            nc.vector.tensor_tensor(out=flat(qT), in0=flat(T[("gate", t, "i")]), in1=flat(T[("gate", t, "g")]), op=ALU.mult)
+            qT = T[("gate", t, "f")]
+            product(eng)(out=flat(qT), in0=flat(T[("gate", t, "i")]), in1=flat(T[("gate", t, "g")]), op=ALU.mult)
             T[("qT", t)] = qT
 
         def e_p(eng, t):
@@ -374,7 +378,7 @@ def tile_layernormlstmcell_kernel(
             T[("cb", t)] = cb
 
         def e_ccopy(eng, t):
-            ct = work.tile([P, H], F32, name="ct", bufs=3)
+            ct = work.tile([P, H], F32, name="ct", bufs=4)
             csum = small.tile([P, 1], F32, name="csum")
             nc.scalar.activation(out=ct[:], in_=flat(T[("cb", t)]), func=ACT.Identity, accum_out=csum[:])
             T[("ct", t)] = ct
@@ -423,8 +427,8 @@ def tile_layernormlstmcell_kernel(
             T[("th", t)] = th
 
         def e_h(eng, t):
-            ht = work.tile([P, H], F32, name="ht", bufs=3)
-            nc.vector.tensor_tensor(out=ht[:], in0=T[("og", t)][:], in1=T[("th", t)][:], op=ALU.mult)
+            ht = T[("ct", t + 1)] if eng == "G" else work.tile([P, H], F32, name="ht", bufs=3)
+            product(eng)(out=ht[:], in0=T[("og", t)][:], in1=T[("th", t)][:], op=ALU.mult)
             T[("ht", t)] = ht
 
         def e_stc(eng, t):
@@ -446,11 +450,11 @@ def tile_layernormlstmcell_kernel(
         def d_main(t, mk):
             u, k = unit(t, mk)
             n = 4 * u + k - ACC_BUFS
-            return "main%d_%d" % (u, k), ["xq%d" % t, "wq%d" % mk, "apply%d_%d" % (n // 4, n % 4)]
+            return "main%d_%d" % (u, k), ["xq%d" % t, "wq%d" % mk, "apply%d_%d" % (n // 4, n % 4), "main%d_%d" % ((4 * u + k - 1) // 4, (k - 1) % 4)]
 
         def d_sq(t, mk):
             u, k = unit(t, mk)
-            deps = ["main%d_%d" % (u, k), "nm%d" % u]
+            deps = ["main%d_%d" % (u, k), "nm%d" % u] + (["sq%d_0" % u] if k else [])
             if k == 0:
                 deps.extend(["fwd%d_%s" % (t - S_BUFS, j) for j in GATE])
                 deps.append("uo2%d" % (t - S_BUFS))
@@ -461,7 +465,7 @@ def tile_layernormlstmcell_kernel(
             u, k = unit(t, mk)
             return "apply%d_%d" % (u, k), ["sq%d_%d" % (u, k)]
 
-        RING = {"f": ("p", 2), "i": ("q", 2), "g": ("q", 2)}
+        RING = {"f": ("cb", 2), "i": ("q", 2), "g": ("q", 2)}
         STEPS = {
             "wcopy": (e_wcopy, lambda t, a: ("wcopy%d" % t, ["wq%d" % (t - 4)])),
             "wt": (e_wt, lambda t, a: ("wt%d_%d" % (t, a), [tp_slot("wtc%d_%d" % (t, a))])),
@@ -471,14 +475,14 @@ def tile_layernormlstmcell_kernel(
             "xt": (e_xt, lambda t, a: ("xt%d" % t, ["ld%d" % (t // GRP), tp_slot("xcopy%d" % t)])),
             "xcopy": (e_xcopy, lambda t, a: ("xcopy%d" % t, ["xt%d" % t, "xq%d" % (t - 2)])),
             "xq": (e_xq, lambda t, a: ("xq%d" % t, ["xcopy%d" % t, "main%d_3" % (2 * (t - 4) + 1)])),
-            "mean": (e_mean, lambda t, a: ("mean%d_%d" % unit(t, a), ["xq%d" % t, "wq%d" % a] + (["nm%d" % (unit(t, a)[0] - 1)] if a % 4 == 0 else []))),
+            "mean": (e_mean, lambda t, a: ("mean%d_%d" % unit(t, a), ["xq%d" % t, "wq%d" % a] + ["nm%d" % (unit(t, a)[0] - 1), "mean%d_%d" % ((2 * t * 4 + a - 1) // 4, (a - 1) % 4)])),
             "nm": (e_nm, lambda t, a: ("nm%d" % (2 * t + a), ["mean%d_3" % (2 * t + a), "apply%d_3" % (2 * t + a - 4)])),
             "main": (e_main, d_main),
             "sq": (e_sq, d_sq),
             "apply": (e_apply, d_apply),
-            "red": (e_red, lambda t, a: ("red%d" % (2 * t + a), ["sq%d_3" % (2 * t + a), "r%d" % (2 * t + a - 4)])),
+            "red": (e_red, lambda t, a: ("red%d" % (2 * t + a), ["sq%d_0" % (2 * t + a), "sq%d_1" % (2 * t + a), "sq%d_2" % (2 * t + a), "sq%d_3" % (2 * t + a), "r%d" % (2 * t + a - 4)])),
             "r": (e_r, lambda t, a: ("r%d" % (2 * t + a), ["red%d" % (2 * t + a), "rs%d" % (2 * t + a - 4), "uo2%d" % (t - 3)])),
-            "rs": (e_rs, lambda t, a: ("rs%d" % (2 * t + a), ["r%d" % (2 * t + a), "apply%d_2" % (2 * t + a)])),
+            "rs": (e_rs, lambda t, a: ("rs%d" % (2 * t + a), ["r%d" % (2 * t + a), "apply%d_0" % (2 * t + a), "apply%d_1" % (2 * t + a), "apply%d_2" % (2 * t + a)])),
             "uo": (e_uo, lambda t, a: ("uo%d" % t, ["r%d" % (2 * t), "apply%d_3" % (2 * t), "acto%d" % (t - 3)])),
             "uo2": (e_uo2, lambda t, a: ("uo2%d" % t, ["uo%d" % t, "r%d" % (2 * t + 1), "apply%d_3" % (2 * t + 1)])),
             "LN2": (e_LN2, lambda t, a: ("LN2%d" % t, ["LN%d" % t, "rc%d" % t])),
@@ -489,16 +493,16 @@ def tile_layernormlstmcell_kernel(
             "act": (e_act, lambda t, a: ("act%d_%s" % (t, a), ["bcopy0", "fwd%d_%s" % (t, a), "%s%d" % (RING[a][0], t - RING[a][1])])),
             "cpt": (e_cpt, lambda t, a: ("cpt%d" % t, [tp_slot("p%d" % t)])),
             "cb": (e_cb, lambda t, a: ("cb%d" % t, ["p%d" % t, "q%d" % t, tp_slot("ccopy%d" % t)])),
-            "q": (e_q, lambda t, a: ("q%d" % t, ["act%d_i" % t, "act%d_g" % t, "cb%d" % (t - 2)])),
+            "q": (e_q, lambda t, a: ("q%d" % t, ["act%d_i" % t, "act%d_g" % t, "p%d" % t])),
             "p": (e_p, lambda t, a: ("p%d" % t, ["act%d_f" % t, "cpt%d" % t, "cb%d" % (t - 2)])),
-            "ccopy": (e_ccopy, lambda t, a: ("ccopy%d" % t, ["cb%d" % t, "LN%d" % (t - 3), "cstat%d" % (t - 3), "stc%d" % (t - 3)])),
+            "ccopy": (e_ccopy, lambda t, a: ("ccopy%d" % t, ["cb%d" % t, "LN%d" % (t - 4), "cstat%d" % (t - 4), "stc%d" % (t - 4), "sth%d" % (t - 5)])),
             "nmc": (e_nmc, lambda t, a: ("nmc%d" % t, ["ccopy%d" % t, "LN%d" % (t - 4)])),
             "cstat": (e_cstat, lambda t, a: ("cstat%d" % t, ["nmc%d" % t, "rc%d" % (t - 4)])),
             "varc": (e_varc, lambda t, a: ("varc%d" % t, ["cstat%d" % t, "rc%d" % (t - 4)])),
             "rc": (e_rc, lambda t, a: ("rc%d" % t, ["varc%d" % t, "LN2%d" % (t - 4)])),
             "LN": (e_LN, lambda t, a: ("LN%d" % t, ["nmc%d" % t, "tanh%d" % (t - 2)])),
             "tanh": (e_tanh, lambda t, a: ("tanh%d" % t, ["LN2%d" % t, "h%d" % (t - 2)])),
-            "h": (e_h, lambda t, a: ("h%d" % t, ["acto%d" % t, "tanh%d" % t, "sth%d" % (t - 3)])),
+            "h": (e_h, lambda t, a: ("h%d" % t, ["acto%d" % t, "tanh%d" % t, "sth%d" % (t - 3)] + (["LN%d" % (t + 1), "cstat%d" % (t + 1), "stc%d" % (t + 1)] if t + 5 < NT else []))),
             "stc": (e_stc, lambda t, a: ("stc%d" % t, ["ccopy%d" % t])),
             "sth": (e_sth, lambda t, a: ("sth%d" % t, ["h%d" % t])),
         }
@@ -529,6 +533,8 @@ def tile_layernormlstmcell_kernel(
                     if t < 0 or t >= NT:
                         continue
                     if op in ("xt", "xcopy", "xq") and t < 2:
+                        continue
+                    if op in ("q", "h") and (eng == "V") != (a >= NT):
                         continue
                     if op == "ld" and (t % GRP != 0 or t < 2 * GRP):
                         continue

from contextlib import ExitStack

import concourse.mybir as mybir
from concourse.masks import make_identity

F32 = mybir.dt.float32
BF16 = mybir.dt.bfloat16
U32 = mybir.dt.uint32
U8 = mybir.dt.uint8
FP8X4 = mybir.dt.float8_e4m3fn_x4
ALU = mybir.AluOpType
ACT = mybir.ActivationFunctionType
AX = mybir.AxisListType

P = 128
B = 2048
K = 512
H = 512
G = 2048
NT = B // P
GRP = 4
EPS = 1e-5
FLOPS = 2 * 2 * B * K * G
GATE = {"i": 0, "f": 1, "g": 2}
TCOLS = 3 * H
ENGINES = ("PE", "S", "V", "G", "SP")
ACC_BUFS = 4
TP_BUFS = 3
S_BUFS = 3

ORDER = {
    "PE": (
        ("xt", 2, None), ("fwd", -2, "g"), ("cpt", -2, None),
        ("mean", 1, 0), ("main", 0, 4), ("mean", 1, 1), ("main", 0, 5), ("mean", 1, 2), ("main", 0, 6), ("mean", 1, 3), ("main", 0, 7),
        ("fwd", -1, "f"),
        ("mean", 1, 4), ("mean", 1, 5), ("mean", 1, 6),
        ("fwd", -1, "i"), ("cb", -2, None),
        ("mean", 1, 7), ("main", 1, 0), ("main", 1, 1), ("main", 1, 2), ("main", 1, 3),
    ),
    "S": (
        ("sq", 0, 0), ("sq", 0, 1), ("sq", 0, 2), ("sq", 0, 3), ("nmc", -3, None), ("act", -2, "g"), ("red", 0, 0), ("cstat", -3, None),
        ("sq", 0, 4), ("sq", 0, 5), ("nm", 1, 0), ("sq", 0, 6), ("acto", -2, None), ("sq", 0, 7), ("varc", -3, None),
        ("act", -1, "f"), ("red", 0, 1), ("act", -1, "i"), ("ccopy", -2, None), ("nm", 1, 1), ("tanh", -4, None),
    ),
    "V": (
        ("apply", 0, 0), ("apply", 0, 1), ("xcopy", 2, None), ("apply", 0, 2), ("apply", 0, 3),
        ("rs", -1, 1), ("xq", 2, None), ("p", -2, None), ("uo2", -1, None), ("q", -2, None),
        ("apply", 0, 4), ("apply", 0, 5), ("apply", 0, 6), ("apply", 0, 7),
        ("LN2", -4, None), ("h", -5, None), ("uo", 0, None), ("rs", 0, 0), ("LN", -3, None),
    ),
    "G": (
        ("h", -5, None), ("r", -1, 1), ("q", -2, None), ("r", 0, 0), ("rc", -3, None),
    ),
    "SP": (
        ("ld", 6, None), ("stc", -2, None), ("sth", -5, None),
    ),
}


def tile_layernormlstmcell_kernel(
    tc, x, h_prev, c_prev, W_ih, W_hh, gamma_ih, beta_ih, gamma_hh, beta_hh, gamma_c, beta_c, out_0, out_1
):
    nc = tc.nc
    x_v = x.rearrange("(p t) k -> p t k", t=NT)
    h_v = h_prev.rearrange("(p t) k -> p t k", t=NT)
    c_v = c_prev.rearrange("(p t) k -> p t k", t=NT)
    ho_v = out_0.rearrange("(p t) k -> p t k", t=NT)
    co_v = out_1.rearrange("(p t) k -> p t k", t=NT)

    with ExitStack() as ctx:
        const = ctx.enter_context(tc.tile_pool(name="const", bufs=1))
        io = ctx.enter_context(tc.tile_pool(name="io", bufs=2))
        xp = ctx.enter_context(tc.tile_pool(name="xp", bufs=4))
        prep = ctx.enter_context(tc.tile_pool(name="prep", bufs=4))
        work = ctx.enter_context(tc.tile_pool(name="work", bufs=2))
        small = ctx.enter_context(tc.tile_pool(name="small", bufs=4))
        ps_acc = ctx.enter_context(tc.psum_pool(name="ps_acc", bufs=ACC_BUFS))
        ps_tp = ctx.enter_context(tc.psum_pool(name="ps_tp", bufs=TP_BUFS))
        ps_mean = ctx.enter_context(tc.psum_pool(name="ps_mean", bufs=1))
        ctx.enter_context(tc.manual_schedule())

        ident = const.tile([P, P], F32, name="ident")
        make_identity(nc, ident[:])
        neghalf = const.tile([P, 1], F32, name="neghalf")
        nc.gpsimd.memset(neghalf[:], -0.5)
        identb = const.tile([P, P], BF16, name="identb")
        nc.vector.tensor_copy(out=identb[:], in_=ident[:])
        junkm = const.tile([P, P], F32, name="junkm")
        junkr = const.tile([P, 8], F32, name="junkr")
        junkv = const.tile([P, P], F32, name="junkv")
        junkc = const.tile([P, H], F32, name="junkc")
        wc = [const.tile([P, G], U32, name="wc%d" % m, align_bytes=64) for m in range(2)]
        ws = [const.tile([P, G], U8, name="ws%d" % m, align_bytes=64) for m in range(2)]
        gam = [const.tile([P, G], BF16, name="gam%d" % m) for m in range(2)]
        gamc = const.tile([P, H], BF16, name="gamc")
        betc = const.tile([P, H], BF16, name="betc")
        cin = const.tile([P, NT, H], BF16, name="cin")
        brow = const.tile([P, P], BF16, name="brow")
        nc.gpsimd.memset(brow[:], 0.0)
        bet = const.tile([P, 12], F32, name="bet")
        bso = const.tile([P, H], F32, name="bso")

        T = {}

        def load_group(g):
            for nm_, view in (("xin", x_v), ("hin", h_v)):
                til = io.tile([P, GRP, K], BF16, name=nm_)
                nc.sync.dma_start(out=til[:], in_=view[:, g * GRP:(g + 1) * GRP, :])
                T[(nm_, g)] = til

        raws = {}
        for u in range(2):
            raws[u] = prep.tile([P, 4, 512], BF16, name="raw0", bufs=2)
        nc.sync.dma_start(out=raws[0][:], in_=W_ih[:, 0:512].rearrange("(p e) c -> p e c", e=4))
        first = {}
        for nm_, view in (("xin", x_v), ("hin", h_v)):
            first[nm_] = io.tile([P, GRP, K], BF16, name=nm_)
            nc.sync.dma_start(out=first[nm_][:, 0:2, :], in_=view[:, 0:2, :])
            T[(nm_, 0)] = first[nm_]
        nc.sync.dma_start(out=raws[1][:], in_=W_ih[:, 512:1024].rearrange("(p e) c -> p e c", e=4))
        for m, W in enumerate((W_ih, W_hh)):
            for hf in range(2):
                if m == 0 and hf == 0:
                    continue
                raw = prep.tile([P, 4, 1024], BF16, name="raw", bufs=3)
                nc.sync.dma_start(
                    out=raw[:], in_=W[:, hf * 1024:(hf + 1) * 1024].rearrange("(p e) c -> p e c", e=4)
                )
                for n in range(2):
                    raws[4 * m + 2 * hf + n] = raw[:, :, n * 512:(n + 1) * 512]
        for v, vec in enumerate((beta_ih, beta_hh)):
            nc.sync.dma_start(out=brow[12 * v:12 * v + 12, :], in_=vec[0:TCOLS].rearrange("(b c) -> b c", c=P))
        for m in range(2):
            nc.sync.dma_start(out=gam[m][:], in_=(gamma_ih, gamma_hh)[m].partition_broadcast(P))
        bo1 = prep.tile([P, H], BF16, name="bo1", bufs=1)
        bo2 = prep.tile([P, H], BF16, name="bo2", bufs=1)
        nc.sync.dma_start(out=bo1[:], in_=beta_ih[TCOLS:G].partition_broadcast(P))
        nc.sync.dma_start(out=bo2[:], in_=beta_hh[TCOLS:G].partition_broadcast(P))
        for nm_, view in (("xin", x_v), ("hin", h_v)):
            nc.sync.dma_start(out=first[nm_][:, 2:GRP, :], in_=view[:, 2:GRP, :])
        nc.sync.dma_start(out=cin[:], in_=c_v)
        load_group(1)
        nc.sync.dma_start(out=gamc[:], in_=gamma_c.partition_broadcast(P))
        nc.sync.dma_start(out=betc[:], in_=beta_c.partition_broadcast(P))

        def e_wcopy(eng, u):
            grp = prep.tile([P, 512, 4], BF16, name="grp", align_bytes=64)
            dst = grp[:].rearrange("p (c i) t -> p c t i", i=4)
            src = (raws[u][:] if u < 2 else raws[u]).rearrange("p t (c i) -> p c t i", i=4)
            if eng == "V":
                nc.vector.tensor_copy(out=dst, in_=src)
            else:
                nc.scalar.copy(out=dst, in_=src)
            T[("grp", u)] = grp

        def e_wt(eng, u, half):
            wt = ps_tp.tile([P, 4, P], F32, name="tp")
            view = flat(wt).bitcast(BF16)
            src = raws[u][:] if u < 2 else raws[u]
            for n in range(2):
                c0 = (2 * half + n) * P
                nc.tensor.matmul(
                    out=view[:, n * 512:(n + 1) * 512], lhsT=identb[:],
                    rhs=src[:, :, c0:c0 + P].rearrange("p t c -> p c t"), start=True, stop=True,
                )
            T[("wt", u, half)] = view

        def e_wtc(eng, u, half):
            if half == 0:
                T[("grp", u)] = prep.tile([P, 512, 4], BF16, name="grp", align_bytes=64)
            nc.scalar.copy(
                out=T[("grp", u)][:, half * 256:half * 256 + 256, :].rearrange("p c t -> p (c t)"), in_=T[("wt", u, half)]
            )

        def e_wq(eng, u):
            m = u // 4
            c0 = (u % 4) * 512
            nc.vector.quantize_mx(
                out=wc[m][:, c0:c0 + 512].bitcast(FP8X4),
                scales=ws[m][:, c0:c0 + 512],
                in_=T[("grp", u)][:].rearrange("p c t -> p (c t)"),
            )

        def e_ld(eng, t):
            load_group(t // GRP)

        def e_xt(eng, t):
            xt = ps_tp.tile([P, 4, P], F32, name="tp")
            for o, nm_ in enumerate(("xin", "hin")):
                src = T[(nm_, t // GRP)]
                words = src[:, t % GRP, :].bitcast(F32)
                for u in range(2):
                    nc.tensor.transpose(xt[:, 2 * o + u, :], words[:, u:2 * P:2], ident[:])
            T[("xt", t)] = xt

        def e_xcopy(eng, t):
            gx = xp.tile([P, 2, P, 2], F32, name="gx", bufs=2, align_bytes=64)
            src = T[("xt", t)][:].rearrange("p (o u) r -> p o r u", u=2)
            if eng == "V":
                nc.vector.tensor_copy(out=gx[:], in_=src)
            else:
                nc.scalar.copy(out=gx[:], in_=src)
            T[("gx", t)] = gx

        def e_xq(eng, t):
            xc = xp.tile([P, 2 * P], U32, name="xc", align_bytes=64)
            xs = xp.tile([P, 2 * P], U8, name="xs", align_bytes=64)
            nc.vector.quantize_mx(
                out=xc[:].bitcast(FP8X4),
                scales=xs[:],
                in_=T[("gx", t)][:].rearrange("p o r u -> p (o r u)").bitcast(BF16),
            )
            T[("xc", t)] = xc
            T[("xs", t)] = xs

        def mx(out, t, m, cols, start, stop):
            nc.tensor.matmul_mx(
                out=out,
                lhsT=T[("xc", t)][:, m * P:(m + 1) * P].bitcast(FP8X4),
                lhsT_scale=T[("xs", t)][:, m * P:(m + 1) * P],
                rhs=wc[m][:, cols].bitcast(FP8X4),
                rhs_scale=ws[m][:, cols],
                start=start,
                stop=stop,
            )

        def e_mean(eng, t, mk):
            m, k = mk // 4, mk % 4
            if k == 0:
                T[("mean", t, m)] = ps_mean.tile([P, P], F32, name="mean_ps")
            for j in range(4 * k, 4 * k + 4):
                mx(T[("mean", t, m)][:], t, m, slice(j * P, (j + 1) * P), j == 0, j == G // P - 1)

        def e_nm(eng, t, m):
            nm = small.tile([P, 1], F32, name="nm")
            if eng == "V":
                nc.vector.tensor_scalar(
                    out=junkv[:], in0=T[("mean", t, m)][:], scalar1=-1.0 / G, scalar2=0.0, op0=ALU.mult, op1=ALU.add,
                    accum_out=nm[:],
                )
            else:
                nc.scalar.activation(
                    out=junkm[:], in_=T[("mean", t, m)][:], func=ACT.Identity, scale=-1.0 / G, accum_out=nm[:]
                )
            T[("nm", t, m)] = nm

        def e_main(eng, t, mk):
            m, k = mk // 4, mk % 4
            acc = ps_acc.tile([P, 512], F32, name="acc")
            mx(acc[:], t, m, slice(k * 512, (k + 1) * 512), True, True)
            T[("acc", t, mk)] = acc

        def e_sq(eng, t, mk):
            m, k = mk // 4, mk % 4
            if k == 0:
                T[("ssq", t, m)] = small.tile([P, 4], F32, name="ssq")
                T[("s", t, m)] = work.tile([P, G], F32, name="s%d" % m, bufs=S_BUFS)
            nc.scalar.activation(
                out=T[("s", t, m)][:, k * 512:(k + 1) * 512], in_=T[("acc", t, mk)][:], func=ACT.Square,
                bias=T[("nm", t, m)][:], scale=1.0, accum_out=T[("ssq", t, m)][:, k:k + 1],
            )

        def e_apply(eng, t, mk):
            m, k = mk // 4, mk % 4
            cols = slice(k * 512, (k + 1) * 512)
            nc.vector.scalar_tensor_tensor(
                out=T[("s", t, m)][:, cols], in0=T[("acc", t, mk)][:], scalar=T[("nm", t, m)][:],
                in1=gam[m][:, cols], op0=ALU.add, op1=ALU.mult,
            )

        def e_red(eng, t, m):
            ssum = small.tile([P, 1], F32, name="ssum")
            nc.scalar.activation(
                out=junkr[:, 4 * m:4 * m + 4], in_=T[("ssq", t, m)][:], func=ACT.Identity, scale=1.0 / G, bias=EPS / 4,
                accum_out=ssum[:],
            )
            T[("ssum", t, m)] = ssum

        def rstd(var, nm_):
            r = small.tile([P, 1], F32, name="r" + nm_, bufs=6)
            nc.gpsimd.tensor_tensor(out=r[:], in0=var[:], in1=neghalf[:], op=ALU.pow)
            return r

        def e_r(eng, t, m):
            T[("r", t, m)] = rstd(T[("ssum", t, m)], "g")

        def e_rs(eng, t, m):
            s = T[("s", t, m)][:, 0:TCOLS]
            r = T[("r", t, m)]
            if eng == "V":
                nc.vector.tensor_scalar(out=s, in0=s, scalar1=r[:], scalar2=None, op0=ALU.mult)
            else:
                nc.scalar.activation(out=s, in_=s, func=ACT.Copy, scale=r[:])

        def e_uo(eng, t):
            if t == 0:
                nc.vector.tensor_tensor(out=bso[:], in0=bo1[:], in1=bo2[:], op=ALU.add)
            uo = work.tile([P, H], F32, name="uo", bufs=3)
            nc.vector.scalar_tensor_tensor(
                out=uo[:], in0=T[("s", t, 0)][:, TCOLS:G], scalar=T[("r", t, 0)][:], in1=bso[:], op0=ALU.mult, op1=ALU.add
            )
            T[("uo", t)] = uo

        def e_uo2(eng, t):
            uo = T[("uo", t)]
            nc.vector.scalar_tensor_tensor(
                out=uo[:], in0=T[("s", t, 1)][:, TCOLS:G], scalar=T[("r", t, 1)][:], in1=uo[:], op0=ALU.mult, op1=ALU.add
            )

        def e_acto(eng, t):
            og = work.tile([P, H], F32, name="og", bufs=5)
            nc.scalar.activation(out=og[:], in_=T[("uo", t)][:], func=ACT.Sigmoid)
            T[("og", t)] = og

        def e_bt(eng, t):
            cols = ps_tp.tile([P, 4, P], F32, name="tp")
            view = flat(cols).bitcast(BF16)
            nc.tensor.transpose(view[:, 0:P], brow[:], identb[:])
            T["bcols"] = view

        def e_bcopy(eng, t):
            half = small.tile([P, 12], F32, name="half")
            nc.vector.tensor_copy(out=half[:], in_=T["bcols"][:, 0:12])
            nc.vector.tensor_tensor(out=bet[:], in0=half[:], in1=T["bcols"][:, 12:24], op=ALU.add)

        def e_fwd(eng, t, j):
            zt = ps_tp.tile([P, 4, P], F32, name="tp")
            T[("zt", t, j)] = zt
            for q in range(4):
                cols = slice((GATE[j] * 4 + q) * P, (GATE[j] * 4 + q + 1) * P)
                for m in range(2):
                    nc.tensor.matmul(
                        out=zt[:, q, :], lhsT=T[("s", t, m)][:, cols], rhs=ident[:], is_transpose=True,
                        start=(m == 0), stop=(m == 1),
                    )

        def e_act(eng, t, j):
            gt = work.tile([P, 4, P], F32, name="gate_" + j)
            for q in range(4):
                b = GATE[j] * 4 + q
                nc.scalar.activation(
                    out=gt[:, q, :], in_=T[("zt", t, j)][:, q, :], func=(ACT.Tanh if j == "g" else ACT.Sigmoid),
                    bias=bet[:, b:b + 1],
                )
            T[("gate", t, j)] = gt

        def flat(til):
            return til[:].rearrange("p q r -> p (q r)")

        def e_cpt(eng, t):
            cp = ps_tp.tile([P, 4, P], F32, name="tp")
            view = flat(cp).bitcast(BF16)
            for q in range(4):
                nc.tensor.transpose(view[:, q * P:(q + 1) * P], cin[:, t, q * P:(q + 1) * P], identb[:])
            T[("cpt", t)] = view[:, 0:H]

        def product(eng):
            return nc.vector.tensor_tensor if eng == "V" else nc.gpsimd.tensor_tensor

        def e_q(eng, t):
            qT = T[("gate", t, "f")]
            product(eng)(out=flat(qT), in0=flat(T[("gate", t, "i")]), in1=flat(T[("gate", t, "g")]), op=ALU.mult)
            T[("qT", t)] = qT

        def e_p(eng, t):
            pT = work.tile([P, 4, P], F32, name="pT")
            nc.vector.tensor_tensor(out=flat(pT), in0=flat(T[("gate", t, "f")]), in1=T[("cpt", t)], op=ALU.mult)
            T[("pT", t)] = pT

        def e_cb(eng, t):
            cb = ps_tp.tile([P, 4, P], F32, name="tp")
            for q in range(4):
                for n, key in enumerate(("pT", "qT")):
                    nc.tensor.matmul(
                        out=cb[:, q, :], lhsT=T[(key, t)][:, q, :], rhs=ident[:], is_transpose=True,
                        start=(n == 0), stop=(n == 1),
                    )
            T[("cb", t)] = cb

        def e_ccopy(eng, t):
            ct = work.tile([P, H], F32, name="ct", bufs=4)
            csum = small.tile([P, 1], F32, name="csum")
            nc.scalar.activation(out=ct[:], in_=flat(T[("cb", t)]), func=ACT.Identity, accum_out=csum[:])
            T[("ct", t)] = ct
            T[("csum", t)] = csum

        def e_nmc(eng, t):
            nmc = small.tile([P, 1], F32, name="nmc")
            if eng == "V":
                nc.vector.tensor_scalar(out=nmc[:], in0=T[("csum", t)][:], scalar1=-1.0 / H, scalar2=None, op0=ALU.mult)
            else:
                nc.scalar.mul(out=nmc[:], in_=T[("csum", t)][:], mul=-1.0 / H)
            T[("nmc", t)] = nmc

        def e_cstat(eng, t):
            ssqc = small.tile([P, 1], F32, name="ssqc")
            nc.scalar.activation(
                out=junkc[:], in_=T[("ct", t)][:], func=ACT.Square, bias=T[("nmc", t)][:], scale=1.0, accum_out=ssqc[:]
            )
            T[("ssqc", t)] = ssqc

        def e_varc(eng, t):
            ssqc = T[("ssqc", t)]
            varc = small.tile([P, 1], F32, name="varc")
            nc.scalar.activation(out=varc[:], in_=ssqc[:], func=ACT.Identity, scale=1.0 / H, bias=EPS)
            T[("varc", t)] = varc

        def e_rc(eng, t):
            T[("rc", t)] = rstd(T[("varc", t)], "c")

        def e_LN(eng, t):
            sc = work.tile([P, H], F32, name="sc")
            nc.vector.scalar_tensor_tensor(
                out=sc[:], in0=T[("ct", t)][:], scalar=T[("nmc", t)][:], in1=gamc[:], op0=ALU.add, op1=ALU.mult
            )
            T[("sc", t)] = sc

        def e_LN2(eng, t):
            sc = T[("sc", t)]
            nc.vector.scalar_tensor_tensor(
                out=sc[:], in0=sc[:], scalar=T[("rc", t)][:], in1=betc[:], op0=ALU.mult, op1=ALU.add
            )

        def e_tanh(eng, t):
            th = work.tile([P, H], F32, name="th")
            nc.scalar.activation(out=th[:], in_=T[("sc", t)][:], func=ACT.Tanh)
            T[("th", t)] = th

        def e_h(eng, t):
            ht = T[("ct", t + 1)] if eng == "G" else work.tile([P, H], F32, name="ht", bufs=3)
            product(eng)(out=ht[:], in0=T[("og", t)][:], in1=T[("th", t)][:], op=ALU.mult)
            T[("ht", t)] = ht

        def e_stc(eng, t):
            nc.sync.dma_start(out=co_v[:, t, :], in_=T[("ct", t)][:])

        def e_sth(eng, t):
            nc.sync.dma_start(out=ho_v[:, t, :], in_=T[("ht", t)][:])

        tp_drains = ["pre"]

        def tp_slot(drain):
            tp_drains.append(drain)
            n = len(tp_drains) - 1
            return tp_drains[n - TP_BUFS] if n >= TP_BUFS else "pre"

        def unit(t, mk):
            return 2 * t + mk // 4, mk % 4

        def d_main(t, mk):
            u, k = unit(t, mk)
            n = 4 * u + k - ACC_BUFS
            return "main%d_%d" % (u, k), ["xq%d" % t, "wq%d" % mk, "apply%d_%d" % (n // 4, n % 4), "main%d_%d" % ((4 * u + k - 1) // 4, (k - 1) % 4)]

        def d_sq(t, mk):
            u, k = unit(t, mk)
            deps = ["main%d_%d" % (u, k), "nm%d" % u] + (["sq%d_0" % u] if k else [])
            if k == 0:
                deps.extend(["fwd%d_%s" % (t - S_BUFS, j) for j in GATE])
                deps.append("uo2%d" % (t - S_BUFS))
                deps.append("red%d" % (u - 4))
            return "sq%d_%d" % (u, k), deps

        def d_apply(t, mk):
            u, k = unit(t, mk)
            return "apply%d_%d" % (u, k), ["sq%d_%d" % (u, k)]

        RING = {"f": ("cb", 2), "i": ("q", 2), "g": ("q", 2)}
        STEPS = {
            "wcopy": (e_wcopy, lambda t, a: ("wcopy%d" % t, ["wq%d" % (t - 4)])),
            "wt": (e_wt, lambda t, a: ("wt%d_%d" % (t, a), [tp_slot("wtc%d_%d" % (t, a))])),
            "wtc": (e_wtc, lambda t, a: ("wtc%d_%d" % (t, a), ["wt%d_%d" % (t, a), "wq%d" % (t - 3)])),
            "wq": (e_wq, lambda t, a: ("wq%d" % t, ["wcopy%d" % t, "wtc%d_1" % t])),
            "ld": (e_ld, lambda t, a: ("ld%d" % (t // GRP), ["xt%d" % (t - GRP - 1)])),
            "xt": (e_xt, lambda t, a: ("xt%d" % t, ["ld%d" % (t // GRP), tp_slot("xcopy%d" % t)])),
            "xcopy": (e_xcopy, lambda t, a: ("xcopy%d" % t, ["xt%d" % t, "xq%d" % (t - 2)])),
            "xq": (e_xq, lambda t, a: ("xq%d" % t, ["xcopy%d" % t, "main%d_3" % (2 * (t - 4) + 1)])),
            "mean": (e_mean, lambda t, a: ("mean%d_%d" % unit(t, a), ["xq%d" % t, "wq%d" % a] + ["nm%d" % (unit(t, a)[0] - 1), "mean%d_%d" % ((2 * t * 4 + a - 1) // 4, (a - 1) % 4)])),
            "nm": (e_nm, lambda t, a: ("nm%d" % (2 * t + a), ["mean%d_3" % (2 * t + a), "apply%d_3" % (2 * t + a - 4)])),
            "main": (e_main, d_main),
            "sq": (e_sq, d_sq),
            "apply": (e_apply, d_apply),
            "red": (e_red, lambda t, a: ("red%d" % (2 * t + a), ["sq%d_0" % (2 * t + a), "sq%d_1" % (2 * t + a), "sq%d_2" % (2 * t + a), "sq%d_3" % (2 * t + a), "r%d" % (2 * t + a - 4)])),
            "r": (e_r, lambda t, a: ("r%d" % (2 * t + a), ["red%d" % (2 * t + a), "rs%d" % (2 * t + a - 4), "uo2%d" % (t - 3)])),
            "rs": (e_rs, lambda t, a: ("rs%d" % (2 * t + a), ["r%d" % (2 * t + a), "apply%d_0" % (2 * t + a), "apply%d_1" % (2 * t + a), "apply%d_2" % (2 * t + a)])),
            "uo": (e_uo, lambda t, a: ("uo%d" % t, ["r%d" % (2 * t), "apply%d_3" % (2 * t), "acto%d" % (t - 3)])),
            "uo2": (e_uo2, lambda t, a: ("uo2%d" % t, ["uo%d" % t, "r%d" % (2 * t + 1), "apply%d_3" % (2 * t + 1)])),
            "LN2": (e_LN2, lambda t, a: ("LN2%d" % t, ["LN%d" % t, "rc%d" % t])),
            "acto": (e_acto, lambda t, a: ("acto%d" % t, ["uo2%d" % t, "h%d" % (t - 5)])),
            "bt": (e_bt, lambda t, a: ("bt0", [tp_slot("bcopy0")])),
            "bcopy": (e_bcopy, lambda t, a: ("bcopy0", ["bt0"])),
            "fwd": (e_fwd, lambda t, a: ("fwd%d_%s" % (t, a), ["rs%d" % (2 * t), "rs%d" % (2 * t + 1), tp_slot("act%d_%s" % (t, a))])),
            "act": (e_act, lambda t, a: ("act%d_%s" % (t, a), ["bcopy0", "fwd%d_%s" % (t, a), "%s%d" % (RING[a][0], t - RING[a][1])])),
            "cpt": (e_cpt, lambda t, a: ("cpt%d" % t, [tp_slot("p%d" % t)])),
            "cb": (e_cb, lambda t, a: ("cb%d" % t, ["p%d" % t, "q%d" % t, tp_slot("ccopy%d" % t)])),
            "q": (e_q, lambda t, a: ("q%d" % t, ["act%d_i" % t, "act%d_g" % t, "p%d" % t])),
            "p": (e_p, lambda t, a: ("p%d" % t, ["act%d_f" % t, "cpt%d" % t, "cb%d" % (t - 2)])),
            "ccopy": (e_ccopy, lambda t, a: ("ccopy%d" % t, ["cb%d" % t, "LN%d" % (t - 4), "cstat%d" % (t - 4), "stc%d" % (t - 4), "sth%d" % (t - 5)])),
            "nmc": (e_nmc, lambda t, a: ("nmc%d" % t, ["ccopy%d" % t, "LN%d" % (t - 4)])),
            "cstat": (e_cstat, lambda t, a: ("cstat%d" % t, ["nmc%d" % t, "rc%d" % (t - 4)])),
            "varc": (e_varc, lambda t, a: ("varc%d" % t, ["cstat%d" % t, "rc%d" % (t - 4)])),
            "rc": (e_rc, lambda t, a: ("rc%d" % t, ["varc%d" % t, "LN2%d" % (t - 4)])),
            "LN": (e_LN, lambda t, a: ("LN%d" % t, ["nmc%d" % t, "tanh%d" % (t - 2)])),
            "tanh": (e_tanh, lambda t, a: ("tanh%d" % t, ["LN2%d" % t, "h%d" % (t - 2)])),
            "h": (e_h, lambda t, a: ("h%d" % t, ["acto%d" % t, "tanh%d" % t, "sth%d" % (t - 3)] + (["LN%d" % (t + 1), "cstat%d" % (t + 1), "stc%d" % (t + 1)] if t + 5 < NT else []))),
            "stc": (e_stc, lambda t, a: ("stc%d" % t, ["ccopy%d" % t])),
            "sth": (e_sth, lambda t, a: ("sth%d" % t, ["h%d" % t])),
        }
        HEAD = {
            "PE": (
                ("xt", 0, None), ("wt", 1, 0), ("wt", 1, 1), ("xt", 1, None), ("wt", 3, 0), ("wt", 3, 1),
                ("wt", 5, 0), ("wt", 5, 1), ("wt", 6, 0), ("wt", 6, 1), ("bt", 0, None),
            ),
            "S": (
                ("xcopy", 0, None), ("wtc", 1, 0), ("wtc", 1, 1), ("xcopy", 1, None), ("wtc", 3, 0), ("wtc", 3, 1),
                ("wtc", 5, 0), ("wtc", 5, 1), ("wtc", 6, 0), ("wtc", 6, 1),
            ),
            "V": (
                ("wcopy", 0, None), ("xq", 0, None), ("wq", 0, None), ("wcopy", 2, None), ("wq", 1, None),
                ("xq", 1, None), ("wq", 2, None), ("wcopy", 4, None), ("wq", 3, None),
                ("wq", 4, None), ("wq", 5, None), ("wcopy", 7, None), ("wq", 6, None), ("wq", 7, None), ("bcopy", 0, None),
            ),
            "G": (),
            "SP": (),
        }

        queues = {}
        for eng in ENGINES:
            todo = list(HEAD[eng])
            for a in range(-3, NT + 9):
                for op, off, arg in ORDER[eng]:
                    t = a + off
                    if t < 0 or t >= NT:
                        continue
                    if op in ("xt", "xcopy", "xq") and t < 2:
                        continue
                    if op in ("q", "h") and (eng == "V") != (a >= NT):
                        continue
                    if op == "ld" and (t % GRP != 0 or t < 2 * GRP):
                        continue
                    todo.append((op, t, arg))
            queues[eng] = []
            for op, t, arg in todo:
                name, deps = STEPS[op][1](t, arg)
                queues[eng].append((name, deps, op, t, arg))

        names = set()
        for eng in ENGINES:
            for item in queues[eng]:
                names.add(item[0])
        done = set()
        at = {eng: 0 for eng in ENGINES}
        left = len(names)
        while left > 0:
            before = left
            for eng in ENGINES:
                while at[eng] < len(queues[eng]):
                    name, deps, op, t, arg = queues[eng][at[eng]]
                    if any(d in names and d not in done for d in deps):
                        break
                    if arg is None:
                        STEPS[op][0](eng, t)
                    else:
                        STEPS[op][0](eng, t, arg)
                    done.add(name)
                    at[eng] += 1
                    left -= 1
            assert left < before, "the per-engine orders wait for each other"
